import numpy as np
import ml_dtypes


def mxq(x, axis, fmt="e4m3"):
    dtype, down = {"e4m3": (ml_dtypes.float8_e4m3fn, 7), "e5m2": (ml_dtypes.float8_e5m2, 14)}[fmt]
    v = np.moveaxis(np.asarray(x, np.float32).astype(ml_dtypes.bfloat16).astype(np.float64), axis, -1)
    blocks = v.reshape(v.shape[:-1] + (-1, 32))
    amax = np.abs(blocks).max(-1, keepdims=True)
    byte = np.maximum(np.where(amax > 0, np.frexp(amax)[1] - 1 + 127, 0) - down, 1)
    scale = np.exp2(byte - 127.0)
    codes = (blocks / scale).astype(np.float32).astype(dtype).astype(np.float64)
    return np.moveaxis((codes * scale).reshape(v.shape), -1, axis)


WIDE = False


def mx_kscale(k):
    if not WIDE:
        return np.ones(k)
    levels = np.array([18, -18])
    if k % 512:
        return np.exp2(np.random.permutation(np.resize(levels, k // 32))).repeat(32)
    a = np.empty((k // 512, 16))
    for p in range(k // 512):
        a[p, :8] = np.random.permutation(np.resize(levels, 8))
        for g in range(8):
            far = levels[np.abs(levels - a[p, g]) >= 10]
            a[p, g + 8] = far[np.random.randint(len(far))]
    return np.exp2(a.ravel()).repeat(32)


BF16 = ml_dtypes.bfloat16


def bf(x):
    return np.asarray(x, np.float32).astype(BF16)


def f64(x):
    return np.asarray(x).astype(np.float64)


B, N, C, DIM, H = 4, 256, 1024, 1024, 8
T = B * N
D = DIM // H // 2
LAYER_NUM = 12
LAM_INIT = 0.8 - 0.6 * np.exp(-0.3 * LAYER_NUM)
SCALE = D ** -0.5


def split_qk(y):
    y = y.reshape(B, N, H, D, 2)
    return np.moveaxis(y, -1, 2).reshape(B, N, 2 * H, D)


def merge_qk(y):
    y = y.reshape(B, N, 2, H, D)
    return np.moveaxis(y, 2, -1).reshape(T, DIM)


def lam_of(lq1, lq2, lk1, lk2):
    return np.exp(np.sum(f64(lq1) * f64(lk1))) - np.exp(np.sum(f64(lq2) * f64(lk2))) + LAM_INIT


def attention_of(yq, yk):
    q = split_qk(yq) * SCALE
    k = split_qk(yk)
    sc = np.stack([(q[:, :, i:i + 1, :] * k).sum(-1) for i in range(2 * H)], axis=2)
    e = np.exp(sc - sc.max(-1, keepdims=True))
    return e / e.sum(-1, keepdims=True)


def setup_inputs():
    s = mx_kscale(T).reshape(B, N, 1)
    u = mx_kscale(DIM)[::32][(5 * np.arange(H)) % (DIM // 32)]
    ucol = np.repeat(u, DIM // H)
    v = mx_kscale(DIM)
    v = v / (np.max(v) * np.max(u))
    ls = 0.45 / D ** 0.25
    x0 = bf(np.random.standard_normal((B, N, C)))
    wq0 = bf(np.random.standard_normal((DIM, C)) / np.sqrt(C))
    wk0 = bf(np.random.standard_normal((DIM, C)) / np.sqrt(C))
    lq1 = bf(np.random.standard_normal(D) * ls)
    lq2 = bf(np.random.standard_normal(D) * ls)
    lk1 = bf(np.random.standard_normal(D) * ls)
    lk2 = bf(np.random.standard_normal(D) * ls)
    yq = f64(x0) @ f64(wq0).T
    yk = f64(x0) @ f64(wk0).T
    att = attention_of(yq, yk)
    g = np.random.standard_normal((B, N, H, H)) * np.exp2(np.random.randint(-6, 1, (B, N, 1, 1))) * 32.0
    g = g / s[:, :, :, None] * u[:, None]
    return {"x": bf(f64(x0) * s),
            "Wq": bf(f64(wq0) / ucol[:, None]),
            "Wk": bf(f64(wk0) * v[:, None]),
            "lq1": lq1,
            "lq2": lq2,
            "lk1": lk1,
            "lk2": lk2,
            "yq": np.asarray(yq, np.float32),
            "yk": np.asarray(yk, np.float32),
            "att": np.asarray(att, np.float32),
            "grad_out": bf(g)}


def reference(x, Wq, Wk, lq1, lq2, lk1, lk2, yq, yk, att, grad_out):
    g = f64(grad_out)
    A = f64(att)
    q = split_qk(f64(yq)) * SCALE
    k = split_qk(f64(yk))
    lam = lam_of(lq1, lq2, lk1, lk2)
    datt = np.zeros((B, N, 2 * H, 2 * H))
    datt[:, :, :H, :H] = g
    datt[:, :, H:, H:] = -lam * g
    dsc = A * (datt - (datt * A).sum(-1, keepdims=True))
    dq = np.stack([(dsc[:, :, i, :, None] * k).sum(2) for i in range(2 * H)], axis=2) * SCALE
    dk = np.stack([(dsc[:, :, :, m, None] * q).sum(2) for m in range(2 * H)], axis=2)
    dyq = merge_qk(dq)
    dyk = merge_qk(dk)
    dy = np.concatenate([dyq, dyk], axis=1)
    w = np.concatenate([f64(Wq), f64(Wk)], axis=0)
    dx = mxq(dy, 1, "e5m2") @ mxq(w, 0, "e4m3")
    xf = f64(x).reshape(T, C)
    dWq = mxq(dyq, 0, "e5m2").T @ mxq(xf, 0, "e4m3")
    return dx.reshape(B, N, C), dWq

@@ -1,0 +1,379 @@
+import math
+from contextlib import ExitStack
+
+import concourse.mybir as mybir
+from concourse.masks import make_identity
+
+F32 = mybir.dt.float32
+BF16 = mybir.dt.bfloat16
+U32 = mybir.dt.uint32
+U8 = mybir.dt.uint8
+E4M3 = mybir.dt.float8_e4m3fn_x4
+E5M2 = mybir.dt.float8_e5m2_x4
+ALU = mybir.AluOpType
+ACT = mybir.ActivationFunctionType
+AXIS_X = mybir.AxisListType.X
+
+P = 128
+T, C, DIM = 1024, 1024, 1024
+D = 64
+SCALE = D ** -0.5
+LAM_INIT = 0.8 - 0.6 * math.exp(-0.3 * 12)
+N_TILE = 512
+CHUNKS = 4
+UNITS = 8
+FLOPS = 2 * T * 2 * DIM * C + 2 * T * DIM * C
+
+
+def tile_differentialattention_pa_v_kernel(
+    tc, x, Wq, Wk, lq1, lq2, lk1, lk2, yq, yk, att, grad_out, out_0, out_1
+):
+    nc = tc.nc
+    with ExitStack() as ctx:
+        keep = ctx.enter_context(tc.tile_pool(name="keep", bufs=1))
+        work = ctx.enter_context(tc.tile_pool(name="work", bufs=2))
+        rows_pool = ctx.enter_context(tc.tile_pool(name="rows", bufs=4))
+        stage = ctx.enter_context(tc.tile_pool(name="stage", bufs=4))
+        prod_psum = ctx.enter_context(tc.psum_pool(name="prod", bufs=3))
+        mx_psum = ctx.enter_context(tc.psum_pool(name="mx", bufs=5))
+        ctx.enter_context(tc.manual_schedule())
+
+        att_v = att.rearrange("B (G a b) i m -> a G B (b i m)", a=4, b=2)
+        g_v = grad_out.rearrange("B (G a b) r h -> a G B (b r h)", a=4, b=2)
+        x_rows = x.rearrange("b n c -> (b n) c")
+        dx_rows = out_0.rearrange("b n c -> (b n) c")
+        dw_rows = out_1.rearrange("(l ph n j) c -> l j ph n c", l=2, ph=2, j=2)
+
+        att_first = keep.tile([P, 1, 512], F32)
+        att_rest = keep.tile([P, CHUNKS - 1, 512], F32)
+        neg_first = keep.tile([P, 1, 2, 2, 64], F32)
+        neg_rest = keep.tile([P, CHUNKS - 1, 2, 2, 64], F32)
+        g_t = keep.tile([P, CHUNKS, 128], BF16)
+
+        def att_of(c):
+            return att_first[:, 0, :] if c == 0 else att_rest[:, c - 1, :]
+
+        def neg_of(c):
+            return neg_first[:, 0] if c == 0 else neg_rest[:, c - 1]
+
+        for a in range(4):
+            nc.sync.dma_start(out=att_first[32 * a : 32 * a + 32, :, :], in_=att_v[a, :, 0:1, :])
+        lvec = []
+        for n, vec in enumerate((lq1, lk1, lq2, lk2)):
+            lt = keep.tile([P, D], BF16, name="lvec%d" % n)
+            nc.scalar.dma_start(out=lt[:], in_=vec.partition_broadcast(P))
+            lvec.append(lt)
+        for a in range(4):
+            nc.gpsimd.dma_start(out=g_t[32 * a : 32 * a + 32, :, :], in_=g_v[a])
+
+        rows_of = {}
+
+        def load_rows(n):
+            if n >= 2 * UNITS:
+                return
+            y, u = (yk, n) if n < UNITS else (yq, n - UNITS)
+            rows = rows_pool.tile([P, 16, 128], F32, name="rows")
+            rows_of[n] = rows
+            flat = y.rearrange("b n c -> (b n c)")
+            base = u * 16 * 8192
+            nc.sync.dma_start(
+                out=rows[0:P:2, :, :],
+                in_=flat[base : base + 16 * 8192].rearrange("(G p c) -> p G c", p=64, c=128),
+            )
+            if u < UNITS - 1:
+                nc.sync.dma_start(
+                    out=rows[1:P:2, :, :],
+                    in_=flat[base + 1 : base + 1 + 16 * 8192].rearrange("(G p c) -> p G c", p=64, c=128),
+                )
+            else:
+                nc.sync.dma_start(
+                    out=rows[1:P:2, 0:15, :],
+                    in_=flat[base + 1 : base + 1 + 15 * 8192].rearrange("(G p c) -> p G c", p=64, c=128),
+                )
+                last = flat[base + 15 * 8192 : base + 16 * 8192].rearrange("(p c) -> p c", c=128)
+                nc.sync.dma_start(out=rows[1:P:2, 15, 0:127], in_=last[:, 1:128])
+
+        load_rows(0)
+        load_rows(1)
+        for a in range(4):
+            nc.sync.dma_start(out=att_rest[32 * a : 32 * a + 32, :, :], in_=att_v[a, :, 1:CHUNKS, :])
+        load_rows(2)
+
+        ident = keep.tile([P, P], F32)
+        make_identity(nc, ident[:])
+
+        warm = keep.tile([P, 1], F32)
+        nc.vector.memset(warm[:], 0.0)
+        warm_out = keep.tile([P, 1], F32)
+        nc.scalar.activation(out=warm_out[:], in_=warm[:], func=ACT.Exp)
+        lprod = keep.tile([P, 2, D], F32)
+        for n in range(2):
+            nc.vector.tensor_tensor(out=lprod[:, n, :], in0=lvec[2 * n][:], in1=lvec[2 * n + 1][:], op=ALU.mult)
+        lsum = keep.tile([P, 2], F32)
+        nc.vector.tensor_reduce(out=lsum[:], in_=lprod[:], axis=AXIS_X, op=ALU.add)
+        lexp = keep.tile([P, 2], F32)
+        nc.scalar.activation(out=lexp[:], in_=lsum[:], func=ACT.Exp)
+        ldiff = keep.tile([P, 1], F32)
+        nc.vector.tensor_tensor(out=ldiff[:], in0=lexp[:, 0:1], in1=lexp[:, 1:2], op=ALU.subtract)
+        lam_scale = keep.tile([P, 1], F32)
+        nc.vector.tensor_scalar(
+            out=lam_scale[:], in0=ldiff[:], scalar1=LAM_INIT, scalar2=SCALE, op0=ALU.add, op1=ALU.mult
+        )
+        g_first = g_t[:, 0, :].rearrange("p (b f) -> p b f", b=2)
+        nc.vector.tensor_scalar(out=neg_first[:, 0, :, 0, :], in0=g_first, scalar1=-SCALE, scalar2=None, op0=ALU.mult)
+        nc.vector.tensor_scalar(
+            out=neg_first[:, 0, :, 1, :], in0=g_first, scalar1=lam_scale[:, 0:1], scalar2=None, op0=ALU.mult
+        )
+        g_rest = g_t[:, 1:CHUNKS, :].rearrange("p c (b f) -> p c b f", b=2)
+        nc.scalar.activation(out=neg_rest[:, :, :, 0, :], in_=g_rest, func=ACT.Copy, scale=-SCALE)
+        nc.scalar.activation(out=neg_rest[:, :, :, 1, :], in_=g_rest, func=ACT.Copy, scale=lam_scale[:, 0:1])
+
+        def diag_views(c, j):
+            nj = neg_of(c)[:, :, j, :].rearrange("p b (r h) -> p b r h", h=8)
+            aj = att_of(c).rearrange("p (b i m) -> p b i m", b=2, i=16)[:, :, 8 * j : 8 * j + 8, 8 * j : 8 * j + 8]
+            return nj, aj
+
+        def dsc_sums(c):
+            for j in range(2):
+                nj, aj = diag_views(c, j)
+                nc.vector.tensor_tensor(out=nj, in0=nj, in1=aj, op=ALU.mult)
+            rsum = work.tile([P, 32], F32, name="rsum")
+            nc.vector.tensor_reduce(
+                out=rsum[:], in_=neg_of(c).rearrange("p b j (r h) -> p (b j r) h", h=8), axis=AXIS_X, op=ALU.add
+            )
+            a3 = att_of(c).rearrange("p (r m) -> p r m", m=16)
+            nc.vector.tensor_tensor(out=a3, in0=a3, in1=rsum[:].unsqueeze(2).to_broadcast([P, 32, 16]), op=ALU.mult)
+
+        def dsc_diag(c):
+            for j in range(2):
+                nj, aj = diag_views(c, j)
+                nc.vector.tensor_tensor(out=aj, in0=aj, in1=nj, op=ALU.subtract)
+
+        def sort_dsc(n):
+            side, c = divmod(n, CHUNKS)
+            srt = work.tile([P, 16, 2, 8, 2], F32, name="srt", align_bytes=64)
+            if side == 0:
+                src = att_of(c).rearrange("p (b i j h) -> p i b h j", b=2, i=16, j=2)
+            else:
+                src = att_of(c).rearrange("p (b j h m) -> p m b h j", b=2, j=2, h=8)
+            if n == 0:
+                nc.vector.tensor_copy(out=srt[:], in_=src)
+            else:
+                nc.scalar.copy(out=srt[:], in_=src)
+            return srt
+
+        def turn_dsc(srt):
+            compact = work.tile([P, 512], F32, name="compact", align_bytes=64)
+            nc.vector.transpose(out=compact[:], in_=srt[:].rearrange("p x b h j -> p (x b h j)"))
+            return compact
+
+        def expand(blocks, compact, tks, g0, g1, on_scalar):
+            src = compact[:].rearrange("p (u e G) -> p e G u", u=4, e=4)[:, :, g0:g1, :]
+            for tk in tks:
+                dst = blocks[:, g0:g1, :, tk, :].rearrange("p G e u -> p e G u")
+                if on_scalar:
+                    nc.scalar.activation(out=dst, in_=src, func=ACT.Copy, scale=mask[:, tk : tk + 1])
+                else:
+                    nc.vector.tensor_scalar(out=dst, in0=src, scalar1=mask[:, tk : tk + 1], scalar2=None, op0=ALU.mult)
+
+        def product_bank(blocks, n, bank):
+            acc = prod_psum.tile([P, 8, 2, 32], F32, name="acc")
+            for gi in range(8):
+                gl = 8 * bank + gi
+                nc.tensor.matmul(
+                    out=acc[:, gi, :, :],
+                    lhsT=blocks[:, 16 * (n % 2) + gl, :, :, :].rearrange("p e t u -> p (e t u)"),
+                    rhs=rows_of[n][:, gl, :].rearrange("p (dd dl j) -> p dl dd j", dl=2, j=2)[:, :, :, 0],
+                    start=True,
+                    stop=True,
+                )
+            return acc
+
+        def turn_bank(turned, bank, acc):
+            nc.vector.transpose(
+                out=turned[:, 512 * bank : 512 * bank + 512], in_=acc[:].rearrange("p g l d -> p (g l d)")
+            )
+
+        def round_unit(turned, dst):
+            nc.scalar.copy(
+                out=dst.rearrange("p l (G tj dl) -> p l G tj dl", tj=16, dl=2),
+                in_=turned[:].rearrange("p (G dl tj l) -> p l G tj dl", dl=2, tj=16, l=2),
+            )
+
+        def quantize(codes, scales, src, fmt):
+            nc.vector.quantize_mx(out=codes.bitcast(fmt), scales=scales, in_=src)
+
+        def load_operand(rows_hbm):
+            raw = work.tile([P, 4, C], BF16, name="raw")
+            nc.sync.dma_start(out=raw[:], in_=rows_hbm.rearrange("(p r) c -> p r c", r=4))
+            return raw
+
+        def interleave(raw, half, pattern, on_scalar):
+            grouped = work.tile([P, N_TILE, 2, 2], BF16, name="grouped", align_bytes=64)
+            src = raw[:, :, half * N_TILE : (half + 1) * N_TILE].rearrange(pattern, j=2)
+            if on_scalar:
+                nc.scalar.copy(out=grouped[:], in_=src)
+            else:
+                nc.vector.tensor_copy(out=grouped[:], in_=src)
+            return grouped
+
+        def quantize_operand(mx, half, grouped):
+            cols = slice(half * N_TILE, (half + 1) * N_TILE)
+            quantize(mx[0][:, cols], mx[1][:, cols], grouped[:].rearrange("p c j l -> p (c j l)"), E4M3)
+
+        def mx_pair(name, width):
+            codes = keep.tile([P, width], U32, name=name + "_codes", align_bytes=64)
+            scales = keep.tile([P, width], U8, name=name + "_scales", align_bytes=64)
+            return codes, scales
+
+        def mx_tile(passes, dst):
+            res = stage.tile([P, C], F32, name="res")
+            for half in range(2):
+                cols = slice(half * N_TILE, (half + 1) * N_TILE)
+                acc = mx_psum.tile([P, N_TILE], F32, name="bank")
+                for n, (lc, ls, rc, rs) in enumerate(passes):
+                    nc.tensor.matmul_mx(
+                        out=acc[:],
+                        lhsT=lc.bitcast(E5M2),
+                        lhsT_scale=ls,
+                        rhs=rc[:, cols].bitcast(E4M3),
+                        rhs_scale=rs[:, cols],
+                        start=(n == 0),
+                        stop=(n == len(passes) - 1),
+                    )
+                nc.scalar.copy(out=res[:, cols], in_=acc[:])
+            nc.sync.dma_start(out=dst, in_=res[:])
+
+        x_mx = [mx_pair("x%d" % g, C) for g in range(2)]
+        w_mx = [mx_pair("w%d" % n, C) for n in range(4)]
+        tok_mx = [mx_pair("tok%d" % g, DIM) for g in range(2)]
+        q_mx = [mx_pair("q%d" % c, 512) for c in range(CHUNKS)]
+        k_mx = [mx_pair("k%d" % u, 256) for u in range(UNITS)]
+        dyq = [keep.tile([P, 2, 2048], BF16, name="dyq%d" % g, align_bytes=64) for g in range(2)]
+        tok = keep.tile([P, 4, 256, 4], BF16, align_bytes=64)
+        dyk = {}
+
+        def token_side(g, l):
+            words = dyq[g][:].rearrange("p l n -> p (l n)").bitcast(F32)
+            for j in range(2):
+                tr = mx_psum.tile([P, 4, P], F32, name="bank")
+                for r in range(4):
+                    nc.tensor.transpose(tr[:, r, :], words[:, 1024 * l + 2 * r + j : 1024 * (l + 1) : 8], ident[:])
+                nc.scalar.copy(
+                    out=tok[:, 2 * l + j, :, :],
+                    in_=tr[:].rearrange("p r n -> p (r n)").bitcast(BF16).rearrange("p (r n) -> p n r", r=4),
+                )
+
+        def quantize_token_side(g, l):
+            cols = slice(512 * l, 512 * l + 512)
+            src = tok[:, 2 * l : 2 * l + 2, :, :].rearrange("p a n r -> p (a n r)")
+            quantize(tok_mx[g][0][:, cols], tok_mx[g][1][:, cols], src, E5M2)
+
+        def quantize_unit(n):
+            if n < UNITS:
+                if n % 2 == 1:
+                    c = n // 2
+                    for l in range(2):
+                        cols = slice(256 * l, 256 * l + 256)
+                        src = dyq[c // 2][:, l, 1024 * (c % 2) : 1024 * (c % 2) + 1024]
+                        quantize(q_mx[c][0][:, cols], q_mx[c][1][:, cols], src, E5M2)
+            else:
+                u = n - UNITS
+                quantize(k_mx[u][0][:], k_mx[u][1][:], dyk[u][:].rearrange("p l n -> p (l n)"), E5M2)
+
+        def dx_tile(u):
+            c, half = divmod(u, 2)
+            passes = []
+            for l in range(2):
+                cols = slice(256 * l + 128 * half, 256 * l + 128 * half + 128)
+                passes.append((q_mx[c][0][:, cols], q_mx[c][1][:, cols]) + w_mx[l])
+            for l in range(2):
+                cols = slice(128 * l, 128 * l + 128)
+                passes.append((k_mx[u][0][:, cols], k_mx[u][1][:, cols]) + w_mx[2 + l])
+            mx_tile(passes, dx_rows[128 * u : 128 * u + 128, :])
+
+        def dw_tile(u):
+            cols = slice(128 * u, 128 * u + 128)
+            passes = [(tok_mx[g][0][:, cols], tok_mx[g][1][:, cols]) + x_mx[g] for g in range(2)]
+            mx_tile(passes, dw_rows[u // 4, (u // 2) % 2, u % 2])
+
+        X_PATTERN = "p (j l) c -> p c j l"
+        W_PATTERN = "p (l j) c -> p c j l"
+        w_rows = [w[512 * l : 512 * l + 512, :] for w in (Wq, Wk) for l in range(2)]
+
+        dsc_sums(0)
+        mask = keep.tile([P, 8], F32)
+        nc.vector.tensor_reduce(
+            out=mask[:], in_=ident[:].rearrange("p (t r) -> p t r", r=16), axis=AXIS_X, op=ALU.add
+        )
+        dsc_diag(0)
+        compact = turn_dsc(sort_dsc(0))
+        blocks = work.tile([P, 32, 4, 8, 4], F32, name="blocks", align_bytes=64)
+        expand(blocks, compact, range(8), 0, 16, False)
+        expand(blocks, compact, range(8), 16, 32, False)
+
+        raw = {}
+        grouped = {}
+        for n in range(2 * UNITS):
+            first = n % 2 == 0
+            nxt = n // 2 + 1
+            prepare = nxt < 2 * CHUNKS
+            load_rows(n + 3)
+            if n in (0, 2):
+                raw["x", n // 2] = load_operand(x_rows[512 * (n // 2) : 512 * (n // 2) + 512, :])
+            turned = work.tile([P, 1024], F32, name="turned", align_bytes=64)
+            acc0 = product_bank(blocks, n, 0)
+            acc1 = product_bank(blocks, n, 1)
+            if first and prepare:
+                if nxt < CHUNKS:
+                    dsc_sums(nxt)
+                    dsc_diag(nxt)
+                srt = sort_dsc(nxt)
+            if not first and prepare:
+                expand(new_blocks, compact, range(0, 3), 0, 32, False)
+            if 8 <= n < 12:
+                grouped["w", 0] = interleave(raw["w", n - 8], 0, W_PATTERN, False)
+            turn_bank(turned, 0, acc0)
+            if 8 <= n < 12:
+                quantize_operand(w_mx[n - 8], 0, grouped["w", 0])
+                grouped["w", 1] = interleave(raw["w", n - 8], 1, W_PATTERN, False)
+            if n > 0:
+                quantize_unit(n - 1)
+            if 3 <= n < 7:
+                quantize_operand(x_mx[(n - 3) // 2], (n - 3) % 2, grouped["x", n - 3])
+            if not first and prepare:
+                expand(new_blocks, compact, range(3, 6 if n < UNITS else 8), 0, 32, False)
+            turn_bank(turned, 1, acc1)
+            if 8 <= n < 12:
+                quantize_operand(w_mx[n - 8], 1, grouped["w", 1])
+            if n in (5, 6, 9, 10):
+                quantize_token_side(n // 8, (n - 1) % 2)
+            if first and prepare:
+                compact = turn_dsc(srt)
+                new_blocks = work.tile([P, 32, 4, 8, 4], F32, name="blocks", align_bytes=64)
+                if n < UNITS:
+                    expand(new_blocks, compact, range(6, 8), 0, 32, True)
+            if n < UNITS:
+                t0 = 512 * (n % 4)
+                round_unit(turned, dyq[n // 4][:, :, t0 : t0 + 512])
+            else:
+                dyk[n - UNITS] = work.tile([P, 2, 512], BF16, name="dyk", align_bytes=64)
+                round_unit(turned, dyk[n - UNITS][:])
+            if 2 <= n < 6:
+                grouped["x", n - 2] = interleave(raw["x", (n - 2) // 2], n % 2, X_PATTERN, True)
+            if n in (4, 5, 8, 9):
+                token_side(n // 8, n % 2)
+            if n in (5, 6, 8, 9):
+                wn = (5, 6, 8, 9).index(n)
+                raw["w", wn] = load_operand(w_rows[wn])
+            if n in (10, 11):
+                for t in range(4):
+                    dw_tile(4 * (n - 10) + t)
+            if n >= 12:
+                dx_tile(2 * (n - 12))
+                if n < 15:
+                    dx_tile(2 * (n - 12) + 1)
+            if not first and prepare:
+                blocks = new_blocks
+        quantize_unit(2 * UNITS - 1)
+        dx_tile(7)

@@ -1,5 +1,6 @@
 import math
 from contextlib import ExitStack
+from functools import partial
 
 import concourse.mybir as mybir
 from concourse.masks import make_identity
@@ -32,7 +33,7 @@ def tile_differentialattention_pa_v_kernel(
     with ExitStack() as ctx:
         keep = ctx.enter_context(tc.tile_pool(name="keep", bufs=1))
         work = ctx.enter_context(tc.tile_pool(name="work", bufs=2))
-        rows_pool = ctx.enter_context(tc.tile_pool(name="rows", bufs=4))
+        rows_pool = ctx.enter_context(tc.tile_pool(name="rows", bufs=3))
         stage = ctx.enter_context(tc.tile_pool(name="stage", bufs=4))
         prod_psum = ctx.enter_context(tc.psum_pool(name="prod", bufs=3))
         mx_psum = ctx.enter_context(tc.psum_pool(name="mx", bufs=5))
@@ -64,7 +65,7 @@ def tile_differentialattention_pa_v_kernel(
             nc.scalar.dma_start(out=lt[:], in_=vec.partition_broadcast(P))
             lvec.append(lt)
         for a in range(4):
-            nc.gpsimd.dma_start(out=g_t[32 * a : 32 * a + 32, :, :], in_=g_v[a])
+            nc.sync.dma_start(out=g_t[32 * a : 32 * a + 32, :, :], in_=g_v[a])
 
         rows_of = {}
 
@@ -97,7 +98,6 @@ def tile_differentialattention_pa_v_kernel(
         load_rows(1)
         for a in range(4):
             nc.sync.dma_start(out=att_rest[32 * a : 32 * a + 32, :, :], in_=att_v[a, :, 1:CHUNKS, :])
-        load_rows(2)
 
         ident = keep.tile([P, P], F32)
         make_identity(nc, ident[:])
@@ -133,18 +133,18 @@ def tile_differentialattention_pa_v_kernel(
             aj = att_of(c).rearrange("p (b i m) -> p b i m", b=2, i=16)[:, :, 8 * j : 8 * j + 8, 8 * j : 8 * j + 8]
             return nj, aj
 
-        def dsc_sums(c):
+        def softmax_backward(c):
+            rsum = work.tile([P, 2, 2, 8], F32, name="rsum")
+            att4 = att_of(c).rearrange("p (b i m) -> p b i m", b=2, i=16)
             for j in range(2):
                 nj, aj = diag_views(c, j)
                 nc.vector.tensor_tensor(out=nj, in0=nj, in1=aj, op=ALU.mult)
-            rsum = work.tile([P, 32], F32, name="rsum")
-            nc.vector.tensor_reduce(
-                out=rsum[:], in_=neg_of(c).rearrange("p b j (r h) -> p (b j r) h", h=8), axis=AXIS_X, op=ALU.add
-            )
-            a3 = att_of(c).rearrange("p (r m) -> p r m", m=16)
-            nc.vector.tensor_tensor(out=a3, in0=a3, in1=rsum[:].unsqueeze(2).to_broadcast([P, 32, 16]), op=ALU.mult)
-
-        def dsc_diag(c):
+            for j in range(2):
+                nc.vector.tensor_reduce(out=rsum[:, j, :, :], in_=diag_views(c, j)[0], axis=AXIS_X, op=ALU.add)
+            for j in range(2):
+                rows_j = att4[:, :, 8 * j : 8 * j + 8, :]
+                sums_j = rsum[:, j, :, :].unsqueeze(3).to_broadcast([P, 2, 8, 16])
+                nc.vector.tensor_tensor(out=rows_j, in0=rows_j, in1=sums_j, op=ALU.mult)
             for j in range(2):
                 nj, aj = diag_views(c, j)
                 nc.vector.tensor_tensor(out=aj, in0=aj, in1=nj, op=ALU.subtract)
@@ -157,7 +157,8 @@ def tile_differentialattention_pa_v_kernel(
             else:
                 src = att_of(c).rearrange("p (b j h m) -> p m b h j", b=2, j=2, h=8)
             if n == 0:
-                nc.vector.tensor_copy(out=srt[:], in_=src)
+                for j in range(2):
+                    nc.vector.tensor_copy(out=srt[:, 8 * j : 8 * j + 8], in_=src[:, 8 * j : 8 * j + 8])
             else:
                 nc.scalar.copy(out=srt[:], in_=src)
             return srt
@@ -187,6 +188,8 @@ def tile_differentialattention_pa_v_kernel(
                     start=True,
                     stop=True,
                 )
+                if mx_queue:
+                    mx_queue.pop(0)()
             return acc
 
         def turn_bank(turned, bank, acc):
@@ -204,12 +207,12 @@ def tile_differentialattention_pa_v_kernel(
             nc.vector.quantize_mx(out=codes.bitcast(fmt), scales=scales, in_=src)
 
         def load_operand(rows_hbm):
-            raw = work.tile([P, 4, C], BF16, name="raw")
+            raw = work.tile([P, 4, C], BF16, name="raw", bufs=2)
             nc.sync.dma_start(out=raw[:], in_=rows_hbm.rearrange("(p r) c -> p r c", r=4))
             return raw
 
         def interleave(raw, half, pattern, on_scalar):
-            grouped = work.tile([P, N_TILE, 2, 2], BF16, name="grouped", align_bytes=64)
+            grouped = work.tile([P, N_TILE, 2, 2], BF16, name="grouped", align_bytes=64, bufs=3)
             src = raw[:, :, half * N_TILE : (half + 1) * N_TILE].rearrange(pattern, j=2)
             if on_scalar:
                 nc.scalar.copy(out=grouped[:], in_=src)
@@ -226,23 +229,35 @@ def tile_differentialattention_pa_v_kernel(
             scales = keep.tile([P, width], U8, name=name + "_scales", align_bytes=64)
             return codes, scales
 
+        mx_queue = []
+
         def mx_tile(passes, dst):
-            res = stage.tile([P, C], F32, name="res")
-            for half in range(2):
+            held = {}
+
+            def one_pass(half, n):
                 cols = slice(half * N_TILE, (half + 1) * N_TILE)
-                acc = mx_psum.tile([P, N_TILE], F32, name="bank")
-                for n, (lc, ls, rc, rs) in enumerate(passes):
-                    nc.tensor.matmul_mx(
-                        out=acc[:],
-                        lhsT=lc.bitcast(E5M2),
-                        lhsT_scale=ls,
-                        rhs=rc[:, cols].bitcast(E4M3),
-                        rhs_scale=rs[:, cols],
-                        start=(n == 0),
-                        stop=(n == len(passes) - 1),
-                    )
-                nc.scalar.copy(out=res[:, cols], in_=acc[:])
-            nc.sync.dma_start(out=dst, in_=res[:])
+                lc, ls, rc, rs = passes[n]
+                if n == 0:
+                    held["acc"] = mx_psum.tile([P, N_TILE], F32, name="bank")
+                nc.tensor.matmul_mx(
+                    out=held["acc"][:],
+                    lhsT=lc.bitcast(E5M2),
+                    lhsT_scale=ls,
+                    rhs=rc[:, cols].bitcast(E4M3),
+                    rhs_scale=rs[:, cols],
+                    start=(n == 0),
+                    stop=(n == len(passes) - 1),
+                )
+                if n == len(passes) - 1:
+                    if half == 0:
+                        held["res"] = stage.tile([P, C], F32, name="res")
+                    nc.scalar.copy(out=held["res"][:, cols], in_=held["acc"][:])
+                    if half == 1:
+                        nc.sync.dma_start(out=dst, in_=held["res"][:])
+
+            for half in range(2):
+                for n in range(len(passes)):
+                    mx_queue.append(partial(one_pass, half, n))
 
         x_mx = [mx_pair("x%d" % g, C) for g in range(2)]
         w_mx = [mx_pair("w%d" % n, C) for n in range(4)]
@@ -253,12 +268,17 @@ def tile_differentialattention_pa_v_kernel(
         tok = keep.tile([P, 4, 256, 4], BF16, align_bytes=64)
         dyk = {}
 
-        def token_side(g, l):
-            words = dyq[g][:].rearrange("p l n -> p (l n)").bitcast(F32)
+        def sort_words(g, l):
+            words = dyq[g][:].rearrange("p l n -> p (l n)").bitcast(F32)[:, 1024 * l : 1024 * (l + 1)]
+            by_slot = work.tile([P, 2, 4, P], F32, name="by_slot")
+            nc.vector.tensor_copy(out=by_slot[:], in_=words.rearrange("p (q r j) -> p j r q", r=4, j=2))
+            return by_slot
+
+        def token_side(by_slot, l):
             for j in range(2):
                 tr = mx_psum.tile([P, 4, P], F32, name="bank")
                 for r in range(4):
-                    nc.tensor.transpose(tr[:, r, :], words[:, 1024 * l + 2 * r + j : 1024 * (l + 1) : 8], ident[:])
+                    nc.tensor.transpose(tr[:, r, :], by_slot[:, j, r, :], ident[:])
                 nc.scalar.copy(
                     out=tok[:, 2 * l + j, :, :],
                     in_=tr[:].rearrange("p r n -> p (r n)").bitcast(BF16).rearrange("p (r n) -> p n r", r=4),
@@ -301,79 +321,94 @@ def tile_differentialattention_pa_v_kernel(
         W_PATTERN = "p (l j) c -> p c j l"
         w_rows = [w[512 * l : 512 * l + 512, :] for w in (Wq, Wk) for l in range(2)]
 
-        dsc_sums(0)
+        softmax_backward(0)
         mask = keep.tile([P, 8], F32)
         nc.vector.tensor_reduce(
             out=mask[:], in_=ident[:].rearrange("p (t r) -> p t r", r=16), axis=AXIS_X, op=ALU.add
         )
-        dsc_diag(0)
         compact = turn_dsc(sort_dsc(0))
         blocks = work.tile([P, 32, 4, 8, 4], F32, name="blocks", align_bytes=64)
-        expand(blocks, compact, range(8), 0, 16, False)
-        expand(blocks, compact, range(8), 16, 32, False)
+        for g0, g1 in ((0, 8), (8, 16), (16, 32)):
+            expand(blocks, compact, range(8), g0, g1, False)
+        softmax_backward(1)
+        srt = sort_dsc(1)
 
-        raw = {}
+        operands = [(x_rows[512 * g : 512 * g + 512, :], X_PATTERN, x_mx[g]) for g in range(2)]
+        operands.extend((w_rows[n], W_PATTERN, w_mx[n]) for n in range(4))
+        load_step = {0: 3, 3: 4, 5: 5, 8: 0, 10: 1}
+        scalar_piece = {1: (2, 0), 2: (2, 1), 3: (3, 0), 4: (3, 1), 5: (4, 0), 8: (5, 1), 9: (0, 0)}
+        vector_piece = {7: [(4, 1)], 9: [(5, 0)], 10: [(0, 1)], 11: [(1, 0), (1, 1)]}
+        sort_step = {4: [(0, 0)], 5: [(0, 1)], 8: [(1, 0)], 9: [(1, 1)]}
+        turn_step = {6: (0, 0), 7: (0, 1), 10: (1, 0), 11: (1, 1)}
+        mx_step = {11: [(dx_tile, 0)], 12: [(dx_tile, 1), (dx_tile, 2)], 13: [(dx_tile, 3), (dw_tile, 0), (dw_tile, 1)], 14: [(dx_tile, 4), (dw_tile, 2), (dw_tile, 3)], 15: [(dw_tile, 4), (dw_tile, 5), (dw_tile, 6), (dw_tile, 7)]}
+        raw = {2: load_operand(operands[2][0])}
         grouped = {}
+        by_slot = {}
         for n in range(2 * UNITS):
             first = n % 2 == 0
-            nxt = n // 2 + 1
-            prepare = nxt < 2 * CHUNKS
-            load_rows(n + 3)
-            if n in (0, 2):
-                raw["x", n // 2] = load_operand(x_rows[512 * (n // 2) : 512 * (n // 2) + 512, :])
+            c = n // 2
+            load_rows(n + 2)
+            if n in turn_step:
+                token_side(by_slot[turn_step[n]], turn_step[n][1])
+            for kind, t in mx_step.get(n, []):
+                kind(t)
             turned = work.tile([P, 1024], F32, name="turned", align_bytes=64)
             acc0 = product_bank(blocks, n, 0)
             acc1 = product_bank(blocks, n, 1)
-            if first and prepare:
-                if nxt < CHUNKS:
-                    dsc_sums(nxt)
-                    dsc_diag(nxt)
-                srt = sort_dsc(nxt)
-            if not first and prepare:
-                expand(new_blocks, compact, range(0, 3), 0, 32, False)
-            if 8 <= n < 12:
-                grouped["w", 0] = interleave(raw["w", n - 8], 0, W_PATTERN, False)
+            if n == 0:
+                compact = turn_dsc(srt)
+            if first and c + 1 < 2 * CHUNKS:
+                new_blocks = work.tile([P, 32, 4, 8, 4], F32, name="blocks", align_bytes=64)
+                n_vec = 7 if n < 10 else 8
+                expand(new_blocks, compact, range(n_vec, 8), 0, 32, True)
+                expand(new_blocks, compact, range(0, 4), 0, 32, False)
+            if not first and c + 2 < 2 * CHUNKS:
+                if c + 2 < CHUNKS:
+                    softmax_backward(c + 2)
+                srt = sort_dsc(c + 2)
+            if n in scalar_piece:
+                op, half = scalar_piece[n]
+                grouped[op, half] = interleave(raw[op], half, operands[op][1], True)
+            if n - 2 in scalar_piece:
+                op, half = scalar_piece[n - 2]
+                quantize_operand(operands[op][2], half, grouped[op, half])
+            pieces = vector_piece.get(n, [])
+            for op, half in pieces[:1]:
+                grouped[op, half] = interleave(raw[op], half, operands[op][1], False)
             turn_bank(turned, 0, acc0)
-            if 8 <= n < 12:
-                quantize_operand(w_mx[n - 8], 0, grouped["w", 0])
-                grouped["w", 1] = interleave(raw["w", n - 8], 1, W_PATTERN, False)
+            for op, half in pieces[:1]:
+                quantize_operand(operands[op][2], half, grouped[op, half])
             if n > 0:
                 quantize_unit(n - 1)
-            if 3 <= n < 7:
-                quantize_operand(x_mx[(n - 3) // 2], (n - 3) % 2, grouped["x", n - 3])
-            if not first and prepare:
-                expand(new_blocks, compact, range(3, 6 if n < UNITS else 8), 0, 32, False)
+            if first and c + 1 < 2 * CHUNKS:
+                expand(new_blocks, compact, range(4, n_vec), 0, 32, False)
+            for g, l in sort_step.get(n, []):
+                by_slot[g, l] = sort_words(g, l)
+            for op, half in pieces[1:]:
+                grouped[op, half] = interleave(raw[op], half, operands[op][1], False)
+                if n - 1 in turn_step and (op, half) == pieces[1]:
+                    quantize_token_side(*turn_step[n - 1])
+                quantize_operand(operands[op][2], half, grouped[op, half])
+            if n - 1 in turn_step and len(pieces) < 2:
+                quantize_token_side(*turn_step[n - 1])
             turn_bank(turned, 1, acc1)
-            if 8 <= n < 12:
-                quantize_operand(w_mx[n - 8], 1, grouped["w", 1])
-            if n in (5, 6, 9, 10):
-                quantize_token_side(n // 8, (n - 1) % 2)
-            if first and prepare:
+            if not first and c + 2 < 2 * CHUNKS:
                 compact = turn_dsc(srt)
-                new_blocks = work.tile([P, 32, 4, 8, 4], F32, name="blocks", align_bytes=64)
-                if n < UNITS:
-                    expand(new_blocks, compact, range(6, 8), 0, 32, True)
             if n < UNITS:
                 t0 = 512 * (n % 4)
                 round_unit(turned, dyq[n // 4][:, :, t0 : t0 + 512])
             else:
                 dyk[n - UNITS] = work.tile([P, 2, 512], BF16, name="dyk", align_bytes=64)
                 round_unit(turned, dyk[n - UNITS][:])
-            if 2 <= n < 6:
-                grouped["x", n - 2] = interleave(raw["x", (n - 2) // 2], n % 2, X_PATTERN, True)
-            if n in (4, 5, 8, 9):
-                token_side(n // 8, n % 2)
-            if n in (5, 6, 8, 9):
-                wn = (5, 6, 8, 9).index(n)
-                raw["w", wn] = load_operand(w_rows[wn])
-            if n in (10, 11):
-                for t in range(4):
-                    dw_tile(4 * (n - 10) + t)
-            if n >= 12:
-                dx_tile(2 * (n - 12))
-                if n < 15:
-                    dx_tile(2 * (n - 12) + 1)
-            if not first and prepare:
+            if n in load_step:
+                raw[load_step[n]] = load_operand(operands[load_step[n]][0])
+            if not first and c + 1 < 2 * CHUNKS:
                 blocks = new_blocks
+        for u in [5, 6]:
+            dx_tile(u)
+        while mx_queue:
+            mx_queue.pop(0)()
         quantize_unit(2 * UNITS - 1)
         dx_tile(7)
+        while mx_queue:
+            mx_queue.pop(0)()

@@ -33,8 +33,8 @@ def tile_differentialattention_pa_v_kernel(
     with ExitStack() as ctx:
         keep = ctx.enter_context(tc.tile_pool(name="keep", bufs=1))
         work = ctx.enter_context(tc.tile_pool(name="work", bufs=2))
-        rows_pool = ctx.enter_context(tc.tile_pool(name="rows", bufs=3))
-        stage = ctx.enter_context(tc.tile_pool(name="stage", bufs=4))
+        rows_pool = ctx.enter_context(tc.tile_pool(name="rows", bufs=4))
+        stage = ctx.enter_context(tc.tile_pool(name="stage", bufs=3))
         prod_psum = ctx.enter_context(tc.psum_pool(name="prod", bufs=3))
         mx_psum = ctx.enter_context(tc.psum_pool(name="mx", bufs=5))
         ctx.enter_context(tc.manual_schedule())
@@ -95,9 +95,10 @@ def tile_differentialattention_pa_v_kernel(
                 nc.sync.dma_start(out=rows[1:P:2, 15, 0:127], in_=last[:, 1:128])
 
         load_rows(0)
-        load_rows(1)
         for a in range(4):
             nc.sync.dma_start(out=att_rest[32 * a : 32 * a + 32, :, :], in_=att_v[a, :, 1:CHUNKS, :])
+        load_rows(1)
+        load_rows(2)
 
         ident = keep.tile([P, P], F32)
         make_identity(nc, ident[:])
@@ -164,50 +165,65 @@ def tile_differentialattention_pa_v_kernel(
             return srt
 
         def turn_dsc(srt):
-            compact = work.tile([P, 512], F32, name="compact", align_bytes=64)
-            nc.vector.transpose(out=compact[:], in_=srt[:].rearrange("p x b h j -> p (x b h j)"))
+            turned_dsc = work.tile([P, 512], F32, name="turned_dsc", align_bytes=64)
+            nc.vector.transpose(out=turned_dsc[:], in_=srt[:].rearrange("p x b h j -> p (x b h j)"))
+            return turned_dsc
+
+        def order_dsc(turned_dsc):
+            compact = work.tile([P, 32, 4, 4], F32, name="compact")
+            nc.vector.tensor_copy(
+                out=compact[:].rearrange("p G e (l j) -> p e G l j", j=2),
+                in_=turned_dsc[:].rearrange("p (j l e G) -> p e G l j", j=2, l=2, e=4),
+            )
             return compact
 
         def expand(blocks, compact, tks, g0, g1, on_scalar):
-            src = compact[:].rearrange("p (u e G) -> p e G u", u=4, e=4)[:, :, g0:g1, :]
+            src = compact[:, g0:g1, :, :]
             for tk in tks:
-                dst = blocks[:, g0:g1, :, tk, :].rearrange("p G e u -> p e G u")
+                dst = blocks[:, g0:g1, :, tk, :]
                 if on_scalar:
                     nc.scalar.activation(out=dst, in_=src, func=ACT.Copy, scale=mask[:, tk : tk + 1])
                 else:
                     nc.vector.tensor_scalar(out=dst, in0=src, scalar1=mask[:, tk : tk + 1], scalar2=None, op0=ALU.mult)
 
-        def product_bank(blocks, n, bank):
-            acc = prod_psum.tile([P, 8, 2, 32], F32, name="acc")
+        def product_bank(blocks, n, bank, rounded):
+            for kind, t in mx_step.get(2 * n + bank, []):
+                kind(t)
+            acc = prod_psum.tile([P, 8, D], F32, name="acc")
             for gi in range(8):
                 gl = 8 * bank + gi
                 nc.tensor.matmul(
-                    out=acc[:, gi, :, :],
+                    out=acc[:, gi, :],
                     lhsT=blocks[:, 16 * (n % 2) + gl, :, :, :].rearrange("p e t u -> p (e t u)"),
-                    rhs=rows_of[n][:, gl, :].rearrange("p (dd dl j) -> p dl dd j", dl=2, j=2)[:, :, :, 0],
+                    rhs=rows_of[n][:, gl, 0:128:2],
                     start=True,
                     stop=True,
                 )
                 if mx_queue:
                     mx_queue.pop(0)()
-            return acc
+            nc.scalar.copy(out=rounded[:, 512 * bank : 512 * bank + 512], in_=acc[:].rearrange("p g d -> p (g d)"))
 
-        def turn_bank(turned, bank, acc):
-            nc.vector.transpose(
-                out=turned[:, 512 * bank : 512 * bank + 512], in_=acc[:].rearrange("p g l d -> p (g l d)")
-            )
+        def turn_unit(rounded):
+            turned = work.tile([P, 512], F32, name="turned", align_bytes=64)
+            nc.vector.transpose(out=turned[:], in_=rounded[:].bitcast(F32))
+            return turned
 
-        def round_unit(turned, dst):
-            nc.scalar.copy(
-                out=dst.rearrange("p l (G tj dl) -> p l G tj dl", tj=16, dl=2),
-                in_=turned[:].rearrange("p (G dl tj l) -> p l G tj dl", dl=2, tj=16, l=2),
+        def place_unit(n, turned):
+            if n < UNITS:
+                dst = dyq[n // 4][:, :, 256 * (n % 4) : 256 * (n % 4) + 256]
+            else:
+                dyk[n - UNITS] = work.tile([P, 2, 256], F32, name="dyk", align_bytes=64)
+                dst = dyk[n - UNITS][:]
+            nc.vector.tensor_copy(
+                out=dst.rearrange("p l (t j) -> p l t j", j=2),
+                in_=turned[:].rearrange("p (t l j) -> p l t j", l=2, j=2),
             )
 
         def quantize(codes, scales, src, fmt):
             nc.vector.quantize_mx(out=codes.bitcast(fmt), scales=scales, in_=src)
 
         def load_operand(rows_hbm):
-            raw = work.tile([P, 4, C], BF16, name="raw", bufs=2)
+            raw = work.tile([P, 4, C], BF16, name="raw")
             nc.sync.dma_start(out=raw[:], in_=rows_hbm.rearrange("(p r) c -> p r c", r=4))
             return raw
 
@@ -230,6 +246,7 @@ def tile_differentialattention_pa_v_kernel(
             return codes, scales
 
         mx_queue = []
+        tail = []
 
         def mx_tile(passes, dst):
             held = {}
@@ -251,8 +268,13 @@ def tile_differentialattention_pa_v_kernel(
                 if n == len(passes) - 1:
                     if half == 0:
                         held["res"] = stage.tile([P, C], F32, name="res")
-                    nc.scalar.copy(out=held["res"][:, cols], in_=held["acc"][:])
-                    if half == 1:
+                    if half == 1 and tail:
+                        nc.vector.tensor_copy(out=held["res"][:, cols], in_=held["acc"][:])
+                    else:
+                        nc.scalar.copy(out=held["res"][:, cols], in_=held["acc"][:])
+                    if tail:
+                        nc.sync.dma_start(out=dst[:, cols], in_=held["res"][:, cols])
+                    elif half == 1:
                         nc.sync.dma_start(out=dst, in_=held["res"][:])
 
             for half in range(2):
@@ -264,12 +286,12 @@ def tile_differentialattention_pa_v_kernel(
         tok_mx = [mx_pair("tok%d" % g, DIM) for g in range(2)]
         q_mx = [mx_pair("q%d" % c, 512) for c in range(CHUNKS)]
         k_mx = [mx_pair("k%d" % u, 256) for u in range(UNITS)]
-        dyq = [keep.tile([P, 2, 2048], BF16, name="dyq%d" % g, align_bytes=64) for g in range(2)]
+        dyq = [keep.tile([P, 2, 1024], F32, name="dyq%d" % g, align_bytes=64) for g in range(2)]
         tok = keep.tile([P, 4, 256, 4], BF16, align_bytes=64)
         dyk = {}
 
         def sort_words(g, l):
-            words = dyq[g][:].rearrange("p l n -> p (l n)").bitcast(F32)[:, 1024 * l : 1024 * (l + 1)]
+            words = dyq[g][:, l, :]
             by_slot = work.tile([P, 2, 4, P], F32, name="by_slot")
             nc.vector.tensor_copy(out=by_slot[:], in_=words.rearrange("p (q r j) -> p j r q", r=4, j=2))
             return by_slot
@@ -295,11 +317,11 @@ def tile_differentialattention_pa_v_kernel(
                     c = n // 2
                     for l in range(2):
                         cols = slice(256 * l, 256 * l + 256)
-                        src = dyq[c // 2][:, l, 1024 * (c % 2) : 1024 * (c % 2) + 1024]
+                        src = dyq[c // 2][:, l, 512 * (c % 2) : 512 * (c % 2) + 512].bitcast(BF16)
                         quantize(q_mx[c][0][:, cols], q_mx[c][1][:, cols], src, E5M2)
             else:
                 u = n - UNITS
-                quantize(k_mx[u][0][:], k_mx[u][1][:], dyk[u][:].rearrange("p l n -> p (l n)"), E5M2)
+                quantize(k_mx[u][0][:], k_mx[u][1][:], dyk[u][:].rearrange("p l n -> p (l n)").bitcast(BF16), E5M2)
 
         def dx_tile(u):
             c, half = divmod(u, 2)
@@ -326,7 +348,7 @@ def tile_differentialattention_pa_v_kernel(
         nc.vector.tensor_reduce(
             out=mask[:], in_=ident[:].rearrange("p (t r) -> p t r", r=16), axis=AXIS_X, op=ALU.add
         )
-        compact = turn_dsc(sort_dsc(0))
+        compact = order_dsc(turn_dsc(sort_dsc(0)))
         blocks = work.tile([P, 32, 4, 8, 4], F32, name="blocks", align_bytes=64)
         for g0, g1 in ((0, 8), (8, 16), (16, 32)):
             expand(blocks, compact, range(8), g0, g1, False)
@@ -335,80 +357,73 @@ def tile_differentialattention_pa_v_kernel(
 
         operands = [(x_rows[512 * g : 512 * g + 512, :], X_PATTERN, x_mx[g]) for g in range(2)]
         operands.extend((w_rows[n], W_PATTERN, w_mx[n]) for n in range(4))
-        load_step = {0: 3, 3: 4, 5: 5, 8: 0, 10: 1}
-        scalar_piece = {1: (2, 0), 2: (2, 1), 3: (3, 0), 4: (3, 1), 5: (4, 0), 8: (5, 1), 9: (0, 0)}
-        vector_piece = {7: [(4, 1)], 9: [(5, 0)], 10: [(0, 1)], 11: [(1, 0), (1, 1)]}
-        sort_step = {4: [(0, 0)], 5: [(0, 1)], 8: [(1, 0)], 9: [(1, 1)]}
-        turn_step = {6: (0, 0), 7: (0, 1), 10: (1, 0), 11: (1, 1)}
-        mx_step = {11: [(dx_tile, 0)], 12: [(dx_tile, 1), (dx_tile, 2)], 13: [(dx_tile, 3), (dw_tile, 0), (dw_tile, 1)], 14: [(dx_tile, 4), (dw_tile, 2), (dw_tile, 3)], 15: [(dw_tile, 4), (dw_tile, 5), (dw_tile, 6), (dw_tile, 7)]}
+        load_step = {0: 3, 3: 4, 5: 5, 7: 0, 9: 1}
+        scalar_piece = {1: (2, 0), 2: (2, 1), 3: (3, 0), 4: (3, 1), 5: (4, 0), 6: (4, 1), 7: (5, 0), 9: (0, 0), 10: (0, 1)}
+        vector_piece = {7: [(5, 1)], 11: [(1, 0)], 12: [(1, 1)]}
+        sort_step = {6: [(0, 0)], 7: [(0, 1)], 9: [(1, 0)], 10: [(1, 1)]}
+        turn_step = {8: (0, 0), 9: (0, 1), 11: (1, 0), 12: (1, 1)}
+        mx_step = {23: [(dx_tile, 0)], 25: [(dx_tile, 1)], 27: [(dx_tile, 2)], 28: [(dw_tile, 0), (dw_tile, 1)], 29: [(dx_tile, 3)], 30: [(dw_tile, 2), (dw_tile, 3)], 31: [(dx_tile, 4)]}
         raw = {2: load_operand(operands[2][0])}
         grouped = {}
         by_slot = {}
+        compact = order_dsc(turn_dsc(srt))
         for n in range(2 * UNITS):
             first = n % 2 == 0
             c = n // 2
-            load_rows(n + 2)
+            build = first and c + 1 < 2 * CHUNKS
+            prepare = not first and c + 2 < 2 * CHUNKS
+            load_rows(n + 3)
             if n in turn_step:
                 token_side(by_slot[turn_step[n]], turn_step[n][1])
-            for kind, t in mx_step.get(n, []):
-                kind(t)
-            turned = work.tile([P, 1024], F32, name="turned", align_bytes=64)
-            acc0 = product_bank(blocks, n, 0)
-            acc1 = product_bank(blocks, n, 1)
-            if n == 0:
-                compact = turn_dsc(srt)
-            if first and c + 1 < 2 * CHUNKS:
+            if build:
                 new_blocks = work.tile([P, 32, 4, 8, 4], F32, name="blocks", align_bytes=64)
-                n_vec = 7 if n < 10 else 8
+                n_vec = 8
                 expand(new_blocks, compact, range(n_vec, 8), 0, 32, True)
                 expand(new_blocks, compact, range(0, 4), 0, 32, False)
-            if not first and c + 2 < 2 * CHUNKS:
+            if prepare:
                 if c + 2 < CHUNKS:
                     softmax_backward(c + 2)
+            previous = rounded if n > 0 else None
+            rounded = work.tile([P, 1024], BF16, name="rounded", align_bytes=64)
+            product_bank(blocks, n, 0, rounded)
+            if prepare:
                 srt = sort_dsc(c + 2)
+            product_bank(blocks, n, 1, rounded)
             if n in scalar_piece:
                 op, half = scalar_piece[n]
                 grouped[op, half] = interleave(raw[op], half, operands[op][1], True)
+            if n > 0:
+                turned = turn_unit(previous)
+            for g, l in sort_step.get(n, []):
+                by_slot[g, l] = sort_words(g, l)
+            if build:
+                expand(new_blocks, compact, range(4, n_vec), 0, 32, False)
             if n - 2 in scalar_piece:
                 op, half = scalar_piece[n - 2]
                 quantize_operand(operands[op][2], half, grouped[op, half])
+            if n > 0:
+                place_unit(n - 1, turned)
+            if prepare:
+                turned_dsc = turn_dsc(srt)
             pieces = vector_piece.get(n, [])
-            for op, half in pieces[:1]:
+            for op, half in pieces:
                 grouped[op, half] = interleave(raw[op], half, operands[op][1], False)
-            turn_bank(turned, 0, acc0)
-            for op, half in pieces[:1]:
-                quantize_operand(operands[op][2], half, grouped[op, half])
+            if n - 1 in turn_step:
+                quantize_token_side(*turn_step[n - 1])
             if n > 0:
                 quantize_unit(n - 1)
-            if first and c + 1 < 2 * CHUNKS:
-                expand(new_blocks, compact, range(4, n_vec), 0, 32, False)
-            for g, l in sort_step.get(n, []):
-                by_slot[g, l] = sort_words(g, l)
-            for op, half in pieces[1:]:
-                grouped[op, half] = interleave(raw[op], half, operands[op][1], False)
-                if n - 1 in turn_step and (op, half) == pieces[1]:
-                    quantize_token_side(*turn_step[n - 1])
+            if prepare:
+                compact = order_dsc(turned_dsc)
+            for op, half in pieces:
                 quantize_operand(operands[op][2], half, grouped[op, half])
-            if n - 1 in turn_step and len(pieces) < 2:
-                quantize_token_side(*turn_step[n - 1])
-            turn_bank(turned, 1, acc1)
-            if not first and c + 2 < 2 * CHUNKS:
-                compact = turn_dsc(srt)
-            if n < UNITS:
-                t0 = 512 * (n % 4)
-                round_unit(turned, dyq[n // 4][:, :, t0 : t0 + 512])
-            else:
-                dyk[n - UNITS] = work.tile([P, 2, 512], BF16, name="dyk", align_bytes=64)
-                round_unit(turned, dyk[n - UNITS][:])
             if n in load_step:
                 raw[load_step[n]] = load_operand(operands[load_step[n]][0])
             if not first and c + 1 < 2 * CHUNKS:
                 blocks = new_blocks
-        for u in [5, 6]:
-            dx_tile(u)
-        while mx_queue:
-            mx_queue.pop(0)()
+        place_unit(2 * UNITS - 1, turn_unit(rounded))
         quantize_unit(2 * UNITS - 1)
-        dx_tile(7)
+        tail.append(1)
+        for kind, t in [(dw_tile, 4), (dw_tile, 5), (dx_tile, 5), (dw_tile, 6), (dw_tile, 7), (dx_tile, 6), (dx_tile, 7)]:
+            kind(t)
         while mx_queue:
             mx_queue.pop(0)()

@@ -20,10 +20,18 @@ T, C, DIM = 1024, 1024, 1024
 D = 64
 SCALE = D ** -0.5
 LAM_INIT = 0.8 - 0.6 * math.exp(-0.3 * 12)
+K_PASS = 512
 N_TILE = 512
 CHUNKS = 4
-UNITS = 8
+TILES = 8
+STEPS = 2 * TILES
+GROUP = 8 * DIM
 FLOPS = 2 * T * 2 * DIM * C + 2 * T * DIM * C
+
+ROWS_AHEAD = 3
+W_FIRST_STEP = 3
+X_FIRST_STEP = 12
+MX_FIRST_BANK = 25
 
 
 def tile_differentialattention_pa_v_kernel(
@@ -33,397 +41,372 @@ def tile_differentialattention_pa_v_kernel(
     with ExitStack() as ctx:
         keep = ctx.enter_context(tc.tile_pool(name="keep", bufs=1))
         work = ctx.enter_context(tc.tile_pool(name="work", bufs=2))
-        rows_pool = ctx.enter_context(tc.tile_pool(name="rows", bufs=4))
+        rows_pool = ctx.enter_context(tc.tile_pool(name="rows", bufs=ROWS_AHEAD + 1))
         stage = ctx.enter_context(tc.tile_pool(name="stage", bufs=3))
-        prod_psum = ctx.enter_context(tc.psum_pool(name="prod", bufs=3))
+        product_psum = ctx.enter_context(tc.psum_pool(name="product", bufs=3))
         mx_psum = ctx.enter_context(tc.psum_pool(name="mx", bufs=5))
         ctx.enter_context(tc.manual_schedule())
 
-        att_v = att.rearrange("B (G a b) i m -> a G B (b i m)", a=4, b=2)
-        g_v = grad_out.rearrange("B (G a b) r h -> a G B (b r h)", a=4, b=2)
-        x_rows = x.rearrange("b n c -> (b n) c")
-        dx_rows = out_0.rearrange("b n c -> (b n) c")
-        dw_rows = out_1.rearrange("(l ph n j) c -> l j ph n c", l=2, ph=2, j=2)
+        att_hbm = att.rearrange("c (G a b) i m -> a G c (b i m)", a=4, b=2)
+        grad_hbm = grad_out.rearrange("c (G a b) r h -> a G c (b r h)", a=4, b=2)
+        att_sb = [keep.tile([P, 512], F32, name="att%d" % c) for c in range(CHUNKS)]
+        grad_sb = keep.tile([P, CHUNKS, 128], BF16)
 
-        att_first = keep.tile([P, 1, 512], F32)
-        att_rest = keep.tile([P, CHUNKS - 1, 512], F32)
-        neg_first = keep.tile([P, 1, 2, 2, 64], F32)
-        neg_rest = keep.tile([P, CHUNKS - 1, 2, 2, 64], F32)
-        g_t = keep.tile([P, CHUNKS, 128], BF16)
-
-        def att_of(c):
-            return att_first[:, 0, :] if c == 0 else att_rest[:, c - 1, :]
-
-        def neg_of(c):
-            return neg_first[:, 0] if c == 0 else neg_rest[:, c - 1]
-
-        for a in range(4):
-            nc.sync.dma_start(out=att_first[32 * a : 32 * a + 32, :, :], in_=att_v[a, :, 0:1, :])
-        lvec = []
-        for n, vec in enumerate((lq1, lk1, lq2, lk2)):
-            lt = keep.tile([P, D], BF16, name="lvec%d" % n)
-            nc.scalar.dma_start(out=lt[:], in_=vec.partition_broadcast(P))
-            lvec.append(lt)
-        for a in range(4):
-            nc.sync.dma_start(out=g_t[32 * a : 32 * a + 32, :, :], in_=g_v[a])
+        def load_att(c):
+            for a in range(4):
+                nc.sync.dma_start(out=att_sb[c][32 * a : 32 * a + 32, :], in_=att_hbm[a, :, c, :])
 
         rows_of = {}
 
         def load_rows(n):
-            if n >= 2 * UNITS:
-                return
-            y, u = (yk, n) if n < UNITS else (yq, n - UNITS)
+            y, tile = (yk, n) if n < TILES else (yq, n - TILES)
             rows = rows_pool.tile([P, 16, 128], F32, name="rows")
             rows_of[n] = rows
             flat = y.rearrange("b n c -> (b n c)")
-            base = u * 16 * 8192
-            nc.sync.dma_start(
-                out=rows[0:P:2, :, :],
-                in_=flat[base : base + 16 * 8192].rearrange("(G p c) -> p G c", p=64, c=128),
-            )
-            if u < UNITS - 1:
-                nc.sync.dma_start(
-                    out=rows[1:P:2, :, :],
-                    in_=flat[base + 1 : base + 1 + 16 * 8192].rearrange("(G p c) -> p G c", p=64, c=128),
-                )
-            else:
-                nc.sync.dma_start(
-                    out=rows[1:P:2, 0:15, :],
-                    in_=flat[base + 1 : base + 1 + 15 * 8192].rearrange("(G p c) -> p G c", p=64, c=128),
-                )
-                last = flat[base + 15 * 8192 : base + 16 * 8192].rearrange("(p c) -> p c", c=128)
-                nc.sync.dma_start(out=rows[1:P:2, 15, 0:127], in_=last[:, 1:128])
+            base = tile * 16 * GROUP
+            whole = 16 if tile < TILES - 1 else 15
+            for j, groups in ((0, 16), (1, whole)):
+                src = flat[base + j : base + j + groups * GROUP].rearrange("(G p c) -> p G c", p=64, c=128)
+                nc.sync.dma_start(out=rows[j:P:2, 0:groups, :], in_=src)
+            if whole < 16:
+                last = flat[base + whole * GROUP : base + 16 * GROUP].rearrange("(p c) -> p c", c=128)
+                nc.sync.dma_start(out=rows[1:P:2, whole, 0:127], in_=last[:, 1:128])
 
-        load_rows(0)
+        load_att(0)
         for a in range(4):
-            nc.sync.dma_start(out=att_rest[32 * a : 32 * a + 32, :, :], in_=att_v[a, :, 1:CHUNKS, :])
+            nc.sync.dma_start(out=grad_sb[32 * a : 32 * a + 32, :, :], in_=grad_hbm[a])
+        load_rows(0)
+        load_att(1)
+        lam_vectors = []
+        for n, vec in enumerate((lq1, lk1, lq2, lk2)):
+            spread = keep.tile([P, D], BF16, name="lam_vector%d" % n)
+            nc.sync.dma_start(out=spread[:], in_=vec.partition_broadcast(P))
+            lam_vectors.append(spread)
         load_rows(1)
+        load_att(2)
         load_rows(2)
+        load_att(3)
 
         ident = keep.tile([P, P], F32)
         make_identity(nc, ident[:])
 
-        warm = keep.tile([P, 1], F32)
-        nc.vector.memset(warm[:], 0.0)
-        warm_out = keep.tile([P, 1], F32)
-        nc.scalar.activation(out=warm_out[:], in_=warm[:], func=ACT.Exp)
-        lprod = keep.tile([P, 2, D], F32)
-        for n in range(2):
-            nc.vector.tensor_tensor(out=lprod[:, n, :], in0=lvec[2 * n][:], in1=lvec[2 * n + 1][:], op=ALU.mult)
-        lsum = keep.tile([P, 2], F32)
-        nc.vector.tensor_reduce(out=lsum[:], in_=lprod[:], axis=AXIS_X, op=ALU.add)
-        lexp = keep.tile([P, 2], F32)
-        nc.scalar.activation(out=lexp[:], in_=lsum[:], func=ACT.Exp)
-        ldiff = keep.tile([P, 1], F32)
-        nc.vector.tensor_tensor(out=ldiff[:], in0=lexp[:, 0:1], in1=lexp[:, 1:2], op=ALU.subtract)
-        lam_scale = keep.tile([P, 1], F32)
-        nc.vector.tensor_scalar(
-            out=lam_scale[:], in0=ldiff[:], scalar1=LAM_INIT, scalar2=SCALE, op0=ALU.add, op1=ALU.mult
-        )
-        g_first = g_t[:, 0, :].rearrange("p (b f) -> p b f", b=2)
-        nc.vector.tensor_scalar(out=neg_first[:, 0, :, 0, :], in0=g_first, scalar1=-SCALE, scalar2=None, op0=ALU.mult)
-        nc.vector.tensor_scalar(
-            out=neg_first[:, 0, :, 1, :], in0=g_first, scalar1=lam_scale[:, 0:1], scalar2=None, op0=ALU.mult
-        )
-        g_rest = g_t[:, 1:CHUNKS, :].rearrange("p c (b f) -> p c b f", b=2)
-        nc.scalar.activation(out=neg_rest[:, :, :, 0, :], in_=g_rest, func=ACT.Copy, scale=-SCALE)
-        nc.scalar.activation(out=neg_rest[:, :, :, 1, :], in_=g_rest, func=ACT.Copy, scale=lam_scale[:, 0:1])
-
-        def diag_views(c, j):
-            nj = neg_of(c)[:, :, j, :].rearrange("p b (r h) -> p b r h", h=8)
-            aj = att_of(c).rearrange("p (b i m) -> p b i m", b=2, i=16)[:, :, 8 * j : 8 * j + 8, 8 * j : 8 * j + 8]
-            return nj, aj
-
         def softmax_backward(c):
-            rsum = work.tile([P, 2, 2, 8], F32, name="rsum")
-            att4 = att_of(c).rearrange("p (b i m) -> p b i m", b=2, i=16)
+            att4 = att_sb[c][:].rearrange("p (b i m) -> p b i m", b=2, i=16)
+            grad3 = grad_sb[:, c, :].rearrange("p (b r h) -> p b r h", b=2, h=8)
+            rowsum = work.tile([P, 2, 2, 8], F32, name="rowsum")
+            weighted = work.tile([P, 2, 2, 8, 8], F32, name="weighted")
+            diagonal = [att4[:, :, 8 * j : 8 * j + 8, 8 * j : 8 * j + 8] for j in range(2)]
             for j in range(2):
-                nj, aj = diag_views(c, j)
-                nc.vector.tensor_tensor(out=nj, in0=nj, in1=aj, op=ALU.mult)
+                nc.vector.tensor_tensor(out=weighted[:, :, j], in0=grad3, in1=diagonal[j], op=ALU.mult)
             for j in range(2):
-                nc.vector.tensor_reduce(out=rsum[:, j, :, :], in_=diag_views(c, j)[0], axis=AXIS_X, op=ALU.add)
+                nc.vector.tensor_reduce(out=rowsum[:, j], in_=weighted[:, :, j], axis=AXIS_X, op=ALU.add)
             for j in range(2):
-                rows_j = att4[:, :, 8 * j : 8 * j + 8, :]
-                sums_j = rsum[:, j, :, :].unsqueeze(3).to_broadcast([P, 2, 8, 16])
-                nc.vector.tensor_tensor(out=rows_j, in0=rows_j, in1=sums_j, op=ALU.mult)
+                half = att4[:, :, 8 * j : 8 * j + 8, :]
+                sums = rowsum[:, j].unsqueeze(3).to_broadcast([P, 2, 8, 16])
+                nc.vector.tensor_tensor(out=half, in0=half, in1=sums, op=ALU.mult)
             for j in range(2):
-                nj, aj = diag_views(c, j)
-                nc.vector.tensor_tensor(out=aj, in0=aj, in1=nj, op=ALU.subtract)
+                nc.vector.tensor_tensor(out=diagonal[j], in0=diagonal[j], in1=weighted[:, :, j], op=ALU.subtract)
 
-        def sort_dsc(n):
-            side, c = divmod(n, CHUNKS)
-            srt = work.tile([P, 16, 2, 8, 2], F32, name="srt", align_bytes=64)
-            if side == 0:
-                src = att_of(c).rearrange("p (b i j h) -> p i b h j", b=2, i=16, j=2)
+        def sort_dsc(pair):
+            c = pair % CHUNKS
+            sorted_dsc = work.tile([P, 16, 2, 8, 2], F32, name="sorted_dsc", align_bytes=64)
+            if pair < CHUNKS:
+                src = att_sb[c][:].rearrange("p (b i j h) -> p i b h j", b=2, i=16, j=2)
             else:
-                src = att_of(c).rearrange("p (b j h m) -> p m b h j", b=2, j=2, h=8)
-            if n == 0:
+                src = att_sb[c][:].rearrange("p (b j h m) -> p m b h j", b=2, j=2, h=8)
+            if pair == 0:
                 for j in range(2):
-                    nc.vector.tensor_copy(out=srt[:, 8 * j : 8 * j + 8], in_=src[:, 8 * j : 8 * j + 8])
+                    nc.vector.tensor_copy(out=sorted_dsc[:, 8 * j : 8 * j + 8], in_=src[:, 8 * j : 8 * j + 8])
             else:
-                nc.scalar.copy(out=srt[:], in_=src)
-            return srt
+                nc.scalar.copy(out=sorted_dsc[:], in_=src)
+            return sorted_dsc
 
-        def turn_dsc(srt):
+        def turn_dsc(sorted_dsc):
             turned_dsc = work.tile([P, 512], F32, name="turned_dsc", align_bytes=64)
-            nc.vector.transpose(out=turned_dsc[:], in_=srt[:].rearrange("p x b h j -> p (x b h j)"))
+            nc.vector.transpose(out=turned_dsc[:], in_=sorted_dsc[:].rearrange("p x b h j -> p (x b h j)"))
             return turned_dsc
 
         def order_dsc(turned_dsc):
-            compact = work.tile([P, 32, 4, 4], F32, name="compact")
+            ordered = work.tile([P, 32, 4, 4], F32, name="ordered")
             nc.vector.tensor_copy(
-                out=compact[:].rearrange("p G e (l j) -> p e G l j", j=2),
+                out=ordered[:].rearrange("p G e (l j) -> p e G l j", j=2),
                 in_=turned_dsc[:].rearrange("p (j l e G) -> p e G l j", j=2, l=2, e=4),
             )
-            return compact
+            return ordered
 
-        def expand(blocks, compact, tks, g0, g1, on_scalar):
-            src = compact[:, g0:g1, :, :]
-            for tk in tks:
-                dst = blocks[:, g0:g1, :, tk, :]
-                if on_scalar:
-                    nc.scalar.activation(out=dst, in_=src, func=ACT.Copy, scale=mask[:, tk : tk + 1])
-                else:
-                    nc.vector.tensor_scalar(out=dst, in0=src, scalar1=mask[:, tk : tk + 1], scalar2=None, op0=ALU.mult)
+        def build_blocks(blocks, ordered, tokens, groups, token_mask):
+            for k in tokens:
+                nc.vector.tensor_scalar(
+                    out=blocks[:, groups, :, k, :],
+                    in0=ordered[:, groups, :, :],
+                    scalar1=token_mask[:, k : k + 1],
+                    scalar2=None,
+                    op0=ALU.mult,
+                )
+
+        def new_blocks():
+            return work.tile([P, 32, 4, 8, 4], F32, name="blocks", align_bytes=64)
+
+        def quantize(mx, cols, src, fmt):
+            nc.vector.quantize_mx(out=mx[0][:, cols].bitcast(fmt), scales=mx[1][:, cols], in_=src)
+
+        def mx_operand(name, width):
+            codes = keep.tile([P, width], U32, name=name + "_codes", align_bytes=64)
+            scales = keep.tile([P, width], U8, name=name + "_scales", align_bytes=64)
+            return codes, scales
+
+        w_mx = [mx_operand("w%d" % n, C) for n in range(4)]
+        x_mx = [mx_operand("x%d" % g, C) for g in range(2)]
+        token_mx = [mx_operand("token%d" % g, DIM) for g in range(2)]
+        dq_mx = [mx_operand("dq%d" % c, 512) for c in range(CHUNKS)]
+        dk_mx = [mx_operand("dk%d" % u, 256) for u in range(TILES)]
+        dyq = [keep.tile([P, 2, 1024], F32, name="dyq%d" % g, align_bytes=64) for g in range(2)]
+        dyk = {}
+        token_side = keep.tile([P, 4, 256, 4], BF16, align_bytes=64)
+
+        x_rows = x.rearrange("b n c -> (b n) c")
+        inputs = [
+            (w[K_PASS * l : K_PASS * (l + 1), :], "p (v u) c -> p c u v", w_mx[2 * n + l])
+            for n, w in enumerate((Wq, Wk))
+            for l in range(2)
+        ]
+        inputs.extend((x_rows[K_PASS * g : K_PASS * (g + 1), :], "p (u v) c -> p c u v", x_mx[g]) for g in range(2))
+        raw = {}
+        grouped = {}
+
+        def load_input(n):
+            raw[n] = work.tile([P, 4, C], BF16, name="raw")
+            nc.sync.dma_start(out=raw[n][:], in_=inputs[n][0].rearrange("(p r) c -> p r c", r=4))
+
+        def interleave(n, half, copy):
+            grouped[n, half] = work.tile([P, N_TILE, 2, 2], BF16, name="grouped", align_bytes=64, bufs=3)
+            src = raw[n][:, :, half * N_TILE : (half + 1) * N_TILE]
+            copy(out=grouped[n, half][:], in_=src.rearrange(inputs[n][1], u=2))
+
+        def quantize_input(n, half):
+            src = grouped[n, half][:].rearrange("p c u v -> p (c u v)")
+            quantize(inputs[n][2], slice(half * N_TILE, (half + 1) * N_TILE), src, E4M3)
+
+        def sort_words(g, l):
+            by_slot = work.tile([P, 2, 4, P], F32, name="by_slot")
+            nc.vector.tensor_copy(out=by_slot[:], in_=dyq[g][:, l, :].rearrange("f (p r j) -> f j r p", r=4, j=2))
+            return by_slot
+
+        def turn_to_tokens(by_slot, l):
+            for j in range(2):
+                bank = mx_psum.tile([P, 4, P], F32, name="bank")
+                for r in range(4):
+                    nc.tensor.transpose(bank[:, r, :], by_slot[:, j, r, :], ident[:])
+                nc.scalar.copy(
+                    out=token_side[:, 2 * l + j, :, :],
+                    in_=bank[:].rearrange("p r n -> p (r n)").bitcast(BF16).rearrange("p (r n) -> p n r", r=4),
+                )
+
+        def quantize_token_side(g, l):
+            src = token_side[:, 2 * l : 2 * l + 2, :, :].rearrange("p j n r -> p (j n r)")
+            quantize(token_mx[g], slice(512 * l, 512 * l + 512), src, E5M2)
+
+        dx_rows = out_0.rearrange("b n c -> (b n) c")
+        dw_rows = out_1.rearrange("(l s n j) c -> l j s n c", l=2, s=2, j=2)
+        held = {}
+
+        def mx_pass(operands, dst, half, n, after_products):
+            cols = slice(half * N_TILE, (half + 1) * N_TILE)
+            lhs, lhs_cols, rhs = operands[n]
+            last = n == len(operands) - 1
+            if n == 0:
+                held["sums"] = mx_psum.tile([P, N_TILE], F32, name="bank")
+            nc.tensor.matmul_mx(
+                out=held["sums"][:],
+                lhsT=lhs[0][:, lhs_cols].bitcast(E5M2),
+                lhsT_scale=lhs[1][:, lhs_cols],
+                rhs=rhs[0][:, cols].bitcast(E4M3),
+                rhs_scale=rhs[1][:, cols],
+                start=(n == 0),
+                stop=last,
+            )
+            if last:
+                if half == 0:
+                    held["result"] = stage.tile([P, C], F32, name="result")
+                copy = nc.vector.tensor_copy if half == 1 and after_products else nc.scalar.copy
+                copy(out=held["result"][:, cols], in_=held["sums"][:])
+                if after_products:
+                    nc.sync.dma_start(out=dst[:, cols], in_=held["result"][:, cols])
+                elif half == 1:
+                    nc.sync.dma_start(out=dst, in_=held["result"][:])
+
+        def passes_of(operands, dst):
+            return [partial(mx_pass, operands, dst, half, n) for half in range(2) for n in range(len(operands))]
+
+        def dx_passes(u):
+            c, second = divmod(u, 2)
+            operands = [(dq_mx[c], slice(256 * l + P * second, 256 * l + P * second + P), w_mx[l]) for l in range(2)]
+            operands.extend((dk_mx[u], slice(P * l, P * l + P), w_mx[2 + l]) for l in range(2))
+            return passes_of(operands, dx_rows[P * u : P * u + P, :])
+
+        def dw_passes(u):
+            operands = [(token_mx[g], slice(P * u, P * u + P), x_mx[g]) for g in range(2)]
+            return passes_of(operands, dw_rows[u // 4, (u // 2) % 2, u % 2])
+
+        mx_queue = []
+        for u in range(TILES):
+            if u >= 4:
+                mx_queue.extend(dw_passes(2 * (u - 4)) + dw_passes(2 * (u - 4) + 1))
+            mx_queue.extend(dx_passes(u))
 
         def product_bank(blocks, n, bank, rounded):
-            for kind, t in mx_step.get(2 * n + bank, []):
-                kind(t)
-            acc = prod_psum.tile([P, 8, D], F32, name="acc")
-            for gi in range(8):
-                gl = 8 * bank + gi
+            sums = product_psum.tile([P, 8, D], F32, name="sums")
+            for slot in range(8):
+                group = 8 * bank + slot
                 nc.tensor.matmul(
-                    out=acc[:, gi, :],
-                    lhsT=blocks[:, 16 * (n % 2) + gl, :, :, :].rearrange("p e t u -> p (e t u)"),
-                    rhs=rows_of[n][:, gl, 0:128:2],
+                    out=sums[:, slot, :],
+                    lhsT=blocks[:, 16 * (n % 2) + group].rearrange("p e k u -> p (e k u)"),
+                    rhs=rows_of[n][:, group, 0:128:2],
                     start=True,
                     stop=True,
                 )
-                if mx_queue:
-                    mx_queue.pop(0)()
-            nc.scalar.copy(out=rounded[:, 512 * bank : 512 * bank + 512], in_=acc[:].rearrange("p g d -> p (g d)"))
+                if 2 * n + bank >= MX_FIRST_BANK:
+                    mx_queue.pop(0)(False)
+            dst = rounded[:, 512 * bank : 512 * bank + 512]
+            src = sums[:].rearrange("p g d -> p (g d)")
+            if n < TILES:
+                nc.scalar.activation(out=dst, in_=src, func=ACT.Copy, scale=row_factor[:, 0:1])
+            else:
+                nc.scalar.copy(out=dst, in_=src)
 
-        def turn_unit(rounded):
+        def turn_tile(rounded):
             turned = work.tile([P, 512], F32, name="turned", align_bytes=64)
             nc.vector.transpose(out=turned[:], in_=rounded[:].bitcast(F32))
             return turned
 
-        def place_unit(n, turned):
-            if n < UNITS:
+        def place_tile(n, turned):
+            if n < TILES:
                 dst = dyq[n // 4][:, :, 256 * (n % 4) : 256 * (n % 4) + 256]
             else:
-                dyk[n - UNITS] = work.tile([P, 2, 256], F32, name="dyk", align_bytes=64)
-                dst = dyk[n - UNITS][:]
+                dyk[n - TILES] = work.tile([P, 2, 256], F32, name="dyk", align_bytes=64)
+                dst = dyk[n - TILES][:]
             nc.vector.tensor_copy(
                 out=dst.rearrange("p l (t j) -> p l t j", j=2),
                 in_=turned[:].rearrange("p (t l j) -> p l t j", l=2, j=2),
             )
 
-        def quantize(codes, scales, src, fmt):
-            nc.vector.quantize_mx(out=codes.bitcast(fmt), scales=scales, in_=src)
-
-        def load_operand(rows_hbm):
-            raw = work.tile([P, 4, C], BF16, name="raw")
-            nc.sync.dma_start(out=raw[:], in_=rows_hbm.rearrange("(p r) c -> p r c", r=4))
-            return raw
-
-        def interleave(raw, half, pattern, on_scalar):
-            grouped = work.tile([P, N_TILE, 2, 2], BF16, name="grouped", align_bytes=64, bufs=3)
-            src = raw[:, :, half * N_TILE : (half + 1) * N_TILE].rearrange(pattern, j=2)
-            if on_scalar:
-                nc.scalar.copy(out=grouped[:], in_=src)
-            else:
-                nc.vector.tensor_copy(out=grouped[:], in_=src)
-            return grouped
-
-        def quantize_operand(mx, half, grouped):
-            cols = slice(half * N_TILE, (half + 1) * N_TILE)
-            quantize(mx[0][:, cols], mx[1][:, cols], grouped[:].rearrange("p c j l -> p (c j l)"), E4M3)
-
-        def mx_pair(name, width):
-            codes = keep.tile([P, width], U32, name=name + "_codes", align_bytes=64)
-            scales = keep.tile([P, width], U8, name=name + "_scales", align_bytes=64)
-            return codes, scales
-
-        mx_queue = []
-        tail = []
-
-        def mx_tile(passes, dst):
-            held = {}
-
-            def one_pass(half, n):
-                cols = slice(half * N_TILE, (half + 1) * N_TILE)
-                lc, ls, rc, rs = passes[n]
-                if n == 0:
-                    held["acc"] = mx_psum.tile([P, N_TILE], F32, name="bank")
-                nc.tensor.matmul_mx(
-                    out=held["acc"][:],
-                    lhsT=lc.bitcast(E5M2),
-                    lhsT_scale=ls,
-                    rhs=rc[:, cols].bitcast(E4M3),
-                    rhs_scale=rs[:, cols],
-                    start=(n == 0),
-                    stop=(n == len(passes) - 1),
-                )
-                if n == len(passes) - 1:
-                    if half == 0:
-                        held["res"] = stage.tile([P, C], F32, name="res")
-                    if half == 1 and tail:
-                        nc.vector.tensor_copy(out=held["res"][:, cols], in_=held["acc"][:])
-                    else:
-                        nc.scalar.copy(out=held["res"][:, cols], in_=held["acc"][:])
-                    if tail:
-                        nc.sync.dma_start(out=dst[:, cols], in_=held["res"][:, cols])
-                    elif half == 1:
-                        nc.sync.dma_start(out=dst, in_=held["res"][:])
-
-            for half in range(2):
-                for n in range(len(passes)):
-                    mx_queue.append(partial(one_pass, half, n))
-
-        x_mx = [mx_pair("x%d" % g, C) for g in range(2)]
-        w_mx = [mx_pair("w%d" % n, C) for n in range(4)]
-        tok_mx = [mx_pair("tok%d" % g, DIM) for g in range(2)]
-        q_mx = [mx_pair("q%d" % c, 512) for c in range(CHUNKS)]
-        k_mx = [mx_pair("k%d" % u, 256) for u in range(UNITS)]
-        dyq = [keep.tile([P, 2, 1024], F32, name="dyq%d" % g, align_bytes=64) for g in range(2)]
-        tok = keep.tile([P, 4, 256, 4], BF16, align_bytes=64)
-        dyk = {}
-
-        def sort_words(g, l):
-            words = dyq[g][:, l, :]
-            by_slot = work.tile([P, 2, 4, P], F32, name="by_slot")
-            nc.vector.tensor_copy(out=by_slot[:], in_=words.rearrange("p (q r j) -> p j r q", r=4, j=2))
-            return by_slot
-
-        def token_side(by_slot, l):
-            for j in range(2):
-                tr = mx_psum.tile([P, 4, P], F32, name="bank")
-                for r in range(4):
-                    nc.tensor.transpose(tr[:, r, :], by_slot[:, j, r, :], ident[:])
-                nc.scalar.copy(
-                    out=tok[:, 2 * l + j, :, :],
-                    in_=tr[:].rearrange("p r n -> p (r n)").bitcast(BF16).rearrange("p (r n) -> p n r", r=4),
-                )
-
-        def quantize_token_side(g, l):
-            cols = slice(512 * l, 512 * l + 512)
-            src = tok[:, 2 * l : 2 * l + 2, :, :].rearrange("p a n r -> p (a n r)")
-            quantize(tok_mx[g][0][:, cols], tok_mx[g][1][:, cols], src, E5M2)
-
-        def quantize_unit(n):
-            if n < UNITS:
-                if n % 2 == 1:
-                    c = n // 2
-                    for l in range(2):
-                        cols = slice(256 * l, 256 * l + 256)
-                        src = dyq[c // 2][:, l, 512 * (c % 2) : 512 * (c % 2) + 512].bitcast(BF16)
-                        quantize(q_mx[c][0][:, cols], q_mx[c][1][:, cols], src, E5M2)
-            else:
-                u = n - UNITS
-                quantize(k_mx[u][0][:], k_mx[u][1][:], dyk[u][:].rearrange("p l n -> p (l n)").bitcast(BF16), E5M2)
-
-        def dx_tile(u):
-            c, half = divmod(u, 2)
-            passes = []
-            for l in range(2):
-                cols = slice(256 * l + 128 * half, 256 * l + 128 * half + 128)
-                passes.append((q_mx[c][0][:, cols], q_mx[c][1][:, cols]) + w_mx[l])
-            for l in range(2):
-                cols = slice(128 * l, 128 * l + 128)
-                passes.append((k_mx[u][0][:, cols], k_mx[u][1][:, cols]) + w_mx[2 + l])
-            mx_tile(passes, dx_rows[128 * u : 128 * u + 128, :])
-
-        def dw_tile(u):
-            cols = slice(128 * u, 128 * u + 128)
-            passes = [(tok_mx[g][0][:, cols], tok_mx[g][1][:, cols]) + x_mx[g] for g in range(2)]
-            mx_tile(passes, dw_rows[u // 4, (u // 2) % 2, u % 2])
-
-        X_PATTERN = "p (j l) c -> p c j l"
-        W_PATTERN = "p (l j) c -> p c j l"
-        w_rows = [w[512 * l : 512 * l + 512, :] for w in (Wq, Wk) for l in range(2)]
+        def quantize_tile(n):
+            if n >= TILES:
+                src = dyk[n - TILES][:].rearrange("p l n -> p (l n)").bitcast(BF16)
+                quantize(dk_mx[n - TILES], slice(0, 256), src, E5M2)
+            elif n % 2 == 1:
+                c = n // 2
+                for l in range(2):
+                    src = dyq[c // 2][:, l, 512 * (c % 2) : 512 * (c % 2) + 512].bitcast(BF16)
+                    quantize(dq_mx[c], slice(256 * l, 256 * l + 256), src, E5M2)
 
         softmax_backward(0)
         mask = keep.tile([P, 8], F32)
-        nc.vector.tensor_reduce(
-            out=mask[:], in_=ident[:].rearrange("p (t r) -> p t r", r=16), axis=AXIS_X, op=ALU.add
-        )
-        compact = order_dsc(turn_dsc(sort_dsc(0)))
-        blocks = work.tile([P, 32, 4, 8, 4], F32, name="blocks", align_bytes=64)
-        for g0, g1 in ((0, 8), (8, 16), (16, 32)):
-            expand(blocks, compact, range(8), g0, g1, False)
+        nc.vector.tensor_reduce(out=mask[:], in_=ident[:].rearrange("p (k r) -> p k r", r=16), axis=AXIS_X, op=ALU.add)
+        ordered = order_dsc(turn_dsc(sort_dsc(0)))
+        blocks = new_blocks()
+        build_blocks(blocks, ordered, range(8), slice(0, 8), mask)
+        build_blocks(blocks, ordered, range(8), slice(8, 16), mask)
         softmax_backward(1)
-        srt = sort_dsc(1)
+        sorted_dsc = sort_dsc(1)
 
-        operands = [(x_rows[512 * g : 512 * g + 512, :], X_PATTERN, x_mx[g]) for g in range(2)]
-        operands.extend((w_rows[n], W_PATTERN, w_mx[n]) for n in range(4))
-        load_step = {0: 3, 3: 4, 5: 5, 7: 0, 9: 1}
-        scalar_piece = {1: (2, 0), 2: (2, 1), 3: (3, 0), 4: (3, 1), 5: (4, 0), 6: (4, 1), 7: (5, 0), 9: (0, 0), 10: (0, 1)}
-        vector_piece = {7: [(5, 1)], 11: [(1, 0)], 12: [(1, 1)]}
-        sort_step = {6: [(0, 0)], 7: [(0, 1)], 9: [(1, 0)], 10: [(1, 1)]}
-        turn_step = {8: (0, 0), 9: (0, 1), 11: (1, 0), 12: (1, 1)}
-        mx_step = {23: [(dx_tile, 0)], 25: [(dx_tile, 1)], 27: [(dx_tile, 2)], 28: [(dw_tile, 0), (dw_tile, 1)], 29: [(dx_tile, 3)], 30: [(dw_tile, 2), (dw_tile, 3)], 31: [(dx_tile, 4)]}
-        raw = {2: load_operand(operands[2][0])}
-        grouped = {}
+        lam_products = keep.tile([P, 2, D], F32)
+        for n in range(2):
+            nc.vector.tensor_tensor(
+                out=lam_products[:, n, :], in0=lam_vectors[2 * n][:], in1=lam_vectors[2 * n + 1][:], op=ALU.mult
+            )
+        odd = keep.tile([P, 1], F32)
+        nc.vector.tensor_reduce(out=odd[:], in_=ident[:, 1:P:2], axis=AXIS_X, op=ALU.add)
+        lam_sums = keep.tile([P, 2], F32)
+        nc.vector.tensor_reduce(out=lam_sums[:], in_=lam_products[:], axis=AXIS_X, op=ALU.add)
+        even_factor = keep.tile([P, 1], F32)
+        nc.vector.tensor_scalar(out=even_factor[:], in0=odd[:], scalar1=-1.0, scalar2=SCALE, op0=ALU.add, op1=ALU.mult)
+        lam_exps = keep.tile([P, 2], F32)
+        nc.scalar.activation(out=lam_exps[:], in_=lam_sums[:], func=ACT.Exp)
+        build_blocks(blocks, ordered, range(8), slice(16, 32), mask)
+        turned_dsc = turn_dsc(sorted_dsc)
+        lam_difference = keep.tile([P, 1], F32)
+        nc.vector.tensor_tensor(out=lam_difference[:], in0=lam_exps[:, 0:1], in1=lam_exps[:, 1:2], op=ALU.subtract)
+        ordered = order_dsc(turned_dsc)
+        lam_scale = keep.tile([P, 1], F32)
+        nc.vector.tensor_scalar(
+            out=lam_scale[:], in0=lam_difference[:], scalar1=LAM_INIT, scalar2=SCALE, op0=ALU.add, op1=ALU.mult
+        )
+        row_factor = keep.tile([P, 1], F32)
+        nc.vector.scalar_tensor_tensor(
+            out=row_factor[:], in0=odd[:], scalar=lam_scale[:, 0:1], in1=even_factor[:], op0=ALU.mult, op1=ALU.add
+        )
+        scaled_mask = keep.tile([P, 8], F32)
+        nc.vector.tensor_scalar(out=scaled_mask[:], in0=mask[:], scalar1=row_factor[:, 0:1], scalar2=None, op0=ALU.mult)
+
+        sort_at = {4 * g + 5 + l: (g, l) for g in range(2) for l in range(2)}
+        turn_at = {n + 2: piece for n, piece in sort_at.items()}
+        on_scalar = {}
+        on_vector = {}
+        for piece in range(8):
+            n = W_FIRST_STEP + piece
+            if n in turn_at:
+                on_vector[n] = [divmod(piece, 2)]
+            else:
+                on_scalar[n] = divmod(piece, 2)
+        for g in range(2):
+            on_vector[X_FIRST_STEP + g] = [(4 + g, 0), (4 + g, 1)]
+        load_at = {W_FIRST_STEP + 2 * n - 2: n for n in range(4)}
+        load_at.update({X_FIRST_STEP + g - 2: 4 + g for g in range(2)})
+
         by_slot = {}
-        compact = order_dsc(turn_dsc(srt))
-        for n in range(2 * UNITS):
-            first = n % 2 == 0
-            c = n // 2
-            build = first and c + 1 < 2 * CHUNKS
-            prepare = not first and c + 2 < 2 * CHUNKS
-            load_rows(n + 3)
-            if n in turn_step:
-                token_side(by_slot[turn_step[n]], turn_step[n][1])
+        all_groups = slice(0, 32)
+        rounded = None
+        for n in range(STEPS):
+            pair = n // 2
+            build = n % 2 == 0 and pair + 1 < TILES
+            prepare = n % 2 == 1 and pair + 2 < TILES
+            if n + ROWS_AHEAD < STEPS:
+                load_rows(n + ROWS_AHEAD)
+            if n in turn_at:
+                turn_to_tokens(by_slot[turn_at[n]], turn_at[n][1])
             if build:
-                new_blocks = work.tile([P, 32, 4, 8, 4], F32, name="blocks", align_bytes=64)
-                n_vec = 8
-                expand(new_blocks, compact, range(n_vec, 8), 0, 32, True)
-                expand(new_blocks, compact, range(0, 4), 0, 32, False)
-            if prepare:
-                if c + 2 < CHUNKS:
-                    softmax_backward(c + 2)
-            previous = rounded if n > 0 else None
+                next_blocks = new_blocks()
+                next_mask = mask if pair + 1 < CHUNKS else scaled_mask
+                build_blocks(next_blocks, ordered, range(0, 4), all_groups, next_mask)
+            if prepare and pair + 2 < CHUNKS:
+                softmax_backward(pair + 2)
+            previous = rounded
             rounded = work.tile([P, 1024], BF16, name="rounded", align_bytes=64)
             product_bank(blocks, n, 0, rounded)
             if prepare:
-                srt = sort_dsc(c + 2)
+                sorted_dsc = sort_dsc(pair + 2)
             product_bank(blocks, n, 1, rounded)
-            if n in scalar_piece:
-                op, half = scalar_piece[n]
-                grouped[op, half] = interleave(raw[op], half, operands[op][1], True)
+            if n in on_scalar:
+                interleave(*on_scalar[n], nc.scalar.copy)
             if n > 0:
-                turned = turn_unit(previous)
-            for g, l in sort_step.get(n, []):
-                by_slot[g, l] = sort_words(g, l)
+                turned = turn_tile(previous)
+            if n in sort_at:
+                by_slot[sort_at[n]] = sort_words(*sort_at[n])
             if build:
-                expand(new_blocks, compact, range(4, n_vec), 0, 32, False)
-            if n - 2 in scalar_piece:
-                op, half = scalar_piece[n - 2]
-                quantize_operand(operands[op][2], half, grouped[op, half])
+                build_blocks(next_blocks, ordered, range(4, 8), all_groups, next_mask)
+            if n - 1 in on_scalar:
+                quantize_input(*on_scalar[n - 1])
             if n > 0:
-                place_unit(n - 1, turned)
+                place_tile(n - 1, turned)
             if prepare:
-                turned_dsc = turn_dsc(srt)
-            pieces = vector_piece.get(n, [])
-            for op, half in pieces:
-                grouped[op, half] = interleave(raw[op], half, operands[op][1], False)
-            if n - 1 in turn_step:
-                quantize_token_side(*turn_step[n - 1])
+                turned_dsc = turn_dsc(sorted_dsc)
+            for piece in on_vector.get(n, []):
+                interleave(*piece, nc.vector.tensor_copy)
+            if n - 1 in turn_at:
+                quantize_token_side(*turn_at[n - 1])
             if n > 0:
-                quantize_unit(n - 1)
+                quantize_tile(n - 1)
             if prepare:
-                compact = order_dsc(turned_dsc)
-            for op, half in pieces:
-                quantize_operand(operands[op][2], half, grouped[op, half])
-            if n in load_step:
-                raw[load_step[n]] = load_operand(operands[load_step[n]][0])
-            if not first and c + 1 < 2 * CHUNKS:
-                blocks = new_blocks
-        place_unit(2 * UNITS - 1, turn_unit(rounded))
-        quantize_unit(2 * UNITS - 1)
-        tail.append(1)
-        for kind, t in [(dw_tile, 4), (dw_tile, 5), (dx_tile, 5), (dw_tile, 6), (dw_tile, 7), (dx_tile, 6), (dx_tile, 7)]:
-            kind(t)
-        while mx_queue:
-            mx_queue.pop(0)()
+                ordered = order_dsc(turned_dsc)
+            for piece in on_vector.get(n, []):
+                quantize_input(*piece)
+            if n in load_at:
+                load_input(load_at[n])
+            if n % 2 == 1:
+                blocks = next_blocks
+
+        place_tile(STEPS - 1, turn_tile(rounded))
+        quantize_tile(STEPS - 1)
+        for remaining in mx_queue:
+            remaining(True)

@@ -76,12 +76,12 @@ def tile_differentialattention_pa_v_kernel(
         for a in range(4):
             nc.sync.dma_start(out=grad_sb[32 * a : 32 * a + 32, :, :], in_=grad_hbm[a])
         load_rows(0)
-        load_att(1)
         lam_vectors = []
         for n, vec in enumerate((lq1, lk1, lq2, lk2)):
             spread = keep.tile([P, D], BF16, name="lam_vector%d" % n)
             nc.sync.dma_start(out=spread[:], in_=vec.partition_broadcast(P))
             lam_vectors.append(spread)
+        load_att(1)
         load_rows(1)
         load_att(2)
         load_rows(2)
@@ -300,44 +300,55 @@ def tile_differentialattention_pa_v_kernel(
                     src = dyq[c // 2][:, l, 512 * (c % 2) : 512 * (c % 2) + 512].bitcast(BF16)
                     quantize(dq_mx[c], slice(256 * l, 256 * l + 256), src, E5M2)
 
-        softmax_backward(0)
         mask = keep.tile([P, 8], F32)
         nc.vector.tensor_reduce(out=mask[:], in_=ident[:].rearrange("p (k r) -> p k r", r=16), axis=AXIS_X, op=ALU.add)
-        ordered = order_dsc(turn_dsc(sort_dsc(0)))
+        odd = keep.tile([P, 1], F32)
+        nc.vector.tensor_reduce(out=odd[:], in_=ident[:, 1:P:2], axis=AXIS_X, op=ALU.add)
+        even_factor = keep.tile([P, 1], F32)
+        nc.vector.tensor_scalar(out=even_factor[:], in0=odd[:], scalar1=-1.0, scalar2=SCALE, op0=ALU.add, op1=ALU.mult)
+
+        softmax_backward(0)
+        sorted_dsc = sort_dsc(0)
+        warm_up = mx_psum.tile([P, N_TILE], F32, name="bank")
+        nc.tensor.matmul(
+            out=warm_up[:],
+            lhsT=ident[:],
+            rhs=sorted_dsc[:].rearrange("p x b h j -> p (x b h j)"),
+            start=True,
+            stop=True,
+        )
+        ordered = order_dsc(turn_dsc(sorted_dsc))
         blocks = new_blocks()
         build_blocks(blocks, ordered, range(8), slice(0, 8), mask)
         build_blocks(blocks, ordered, range(8), slice(8, 16), mask)
-        softmax_backward(1)
-        sorted_dsc = sort_dsc(1)
 
         lam_products = keep.tile([P, 2, D], F32)
         for n in range(2):
             nc.vector.tensor_tensor(
                 out=lam_products[:, n, :], in0=lam_vectors[2 * n][:], in1=lam_vectors[2 * n + 1][:], op=ALU.mult
             )
-        odd = keep.tile([P, 1], F32)
-        nc.vector.tensor_reduce(out=odd[:], in_=ident[:, 1:P:2], axis=AXIS_X, op=ALU.add)
         lam_sums = keep.tile([P, 2], F32)
         nc.vector.tensor_reduce(out=lam_sums[:], in_=lam_products[:], axis=AXIS_X, op=ALU.add)
-        even_factor = keep.tile([P, 1], F32)
-        nc.vector.tensor_scalar(out=even_factor[:], in0=odd[:], scalar1=-1.0, scalar2=SCALE, op0=ALU.add, op1=ALU.mult)
         lam_exps = keep.tile([P, 2], F32)
         nc.scalar.activation(out=lam_exps[:], in_=lam_sums[:], func=ACT.Exp)
-        build_blocks(blocks, ordered, range(8), slice(16, 32), mask)
-        turned_dsc = turn_dsc(sorted_dsc)
+        softmax_backward(1)
+        sorted_dsc = sort_dsc(1)
         lam_difference = keep.tile([P, 1], F32)
         nc.vector.tensor_tensor(out=lam_difference[:], in0=lam_exps[:, 0:1], in1=lam_exps[:, 1:2], op=ALU.subtract)
-        ordered = order_dsc(turned_dsc)
+        build_blocks(blocks, ordered, range(0, 4), slice(16, 32), mask)
         lam_scale = keep.tile([P, 1], F32)
         nc.vector.tensor_scalar(
             out=lam_scale[:], in0=lam_difference[:], scalar1=LAM_INIT, scalar2=SCALE, op0=ALU.add, op1=ALU.mult
         )
+        build_blocks(blocks, ordered, range(4, 8), slice(16, 32), mask)
         row_factor = keep.tile([P, 1], F32)
         nc.vector.scalar_tensor_tensor(
             out=row_factor[:], in0=odd[:], scalar=lam_scale[:, 0:1], in1=even_factor[:], op0=ALU.mult, op1=ALU.add
         )
+        turned_dsc = turn_dsc(sorted_dsc)
         scaled_mask = keep.tile([P, 8], F32)
         nc.vector.tensor_scalar(out=scaled_mask[:], in0=mask[:], scalar1=row_factor[:, 0:1], scalar2=None, op0=ALU.mult)
+        ordered = order_dsc(turned_dsc)
 
         sort_at = {4 * g + 5 + l: (g, l) for g in range(2) for l in range(2)}
         turn_at = {n + 2: piece for n, piece in sort_at.items()}

import math
from contextlib import ExitStack
from functools import partial

import concourse.mybir as mybir
from concourse.masks import make_identity

F32 = mybir.dt.float32
BF16 = mybir.dt.bfloat16
U32 = mybir.dt.uint32
U8 = mybir.dt.uint8
E4M3 = mybir.dt.float8_e4m3fn_x4
E5M2 = mybir.dt.float8_e5m2_x4
ALU = mybir.AluOpType
ACT = mybir.ActivationFunctionType
AXIS_X = mybir.AxisListType.X

P = 128
T, C, DIM = 1024, 1024, 1024
D = 64
SCALE = D ** -0.5
LAM_INIT = 0.8 - 0.6 * math.exp(-0.3 * 12)
K_PASS = 512
N_TILE = 512
CHUNKS = 4
TILES = 8
STEPS = 2 * TILES
GROUP = 8 * DIM
FLOPS = 2 * T * 2 * DIM * C + 2 * T * DIM * C

ROWS_AHEAD = 3
W_FIRST_STEP = 3
X_FIRST_STEP = 12
MX_FIRST_BANK = 25


def tile_differentialattention_pa_v_kernel(
    tc, x, Wq, Wk, lq1, lq2, lk1, lk2, yq, yk, att, grad_out, out_0, out_1
):
    nc = tc.nc
    with ExitStack() as ctx:
        keep = ctx.enter_context(tc.tile_pool(name="keep", bufs=1))
        work = ctx.enter_context(tc.tile_pool(name="work", bufs=2))
        rows_pool = ctx.enter_context(tc.tile_pool(name="rows", bufs=ROWS_AHEAD + 1))
        stage = ctx.enter_context(tc.tile_pool(name="stage", bufs=3))
        product_psum = ctx.enter_context(tc.psum_pool(name="product", bufs=3))
        mx_psum = ctx.enter_context(tc.psum_pool(name="mx", bufs=5))
        ctx.enter_context(tc.manual_schedule())

        att_hbm = att.rearrange("c (G a b) i m -> a G c (b i m)", a=4, b=2)
        grad_hbm = grad_out.rearrange("c (G a b) r h -> a G c (b r h)", a=4, b=2)
        att_sb = [keep.tile([P, 512], F32, name="att%d" % c) for c in range(CHUNKS)]
        grad_sb = keep.tile([P, CHUNKS, 128], BF16)

        def load_att(c):
            for a in range(4):
                nc.sync.dma_start(out=att_sb[c][32 * a : 32 * a + 32, :], in_=att_hbm[a, :, c, :])

        rows_of = {}

        def load_rows(n):
            y, tile = (yk, n) if n < TILES else (yq, n - TILES)
            rows = rows_pool.tile([P, 16, 128], F32, name="rows")
            rows_of[n] = rows
            flat = y.rearrange("b n c -> (b n c)")
            base = tile * 16 * GROUP
            whole = 16 if tile < TILES - 1 else 15
            for j, groups in ((0, 16), (1, whole)):
                src = flat[base + j : base + j + groups * GROUP].rearrange("(G p c) -> p G c", p=64, c=128)
                nc.sync.dma_start(out=rows[j:P:2, 0:groups, :], in_=src)
            if whole < 16:
                last = flat[base + whole * GROUP : base + 16 * GROUP].rearrange("(p c) -> p c", c=128)
                nc.sync.dma_start(out=rows[1:P:2, whole, 0:127], in_=last[:, 1:128])

        load_att(0)
        for a in range(4):
            nc.sync.dma_start(out=grad_sb[32 * a : 32 * a + 32, :, :], in_=grad_hbm[a])
        load_rows(0)
        lam_vectors = []
        for n, vec in enumerate((lq1, lk1, lq2, lk2)):
            spread = keep.tile([P, D], BF16, name="lam_vector%d" % n)
            nc.sync.dma_start(out=spread[:], in_=vec.partition_broadcast(P))
            lam_vectors.append(spread)
        load_att(1)
        load_rows(1)
        load_att(2)
        load_rows(2)
        load_att(3)

        ident = keep.tile([P, P], F32)
        make_identity(nc, ident[:])

        def softmax_backward(c):
            att4 = att_sb[c][:].rearrange("p (b i m) -> p b i m", b=2, i=16)
            grad3 = grad_sb[:, c, :].rearrange("p (b r h) -> p b r h", b=2, h=8)
            rowsum = work.tile([P, 2, 2, 8], F32, name="rowsum")
            weighted = work.tile([P, 2, 2, 8, 8], F32, name="weighted")
            diagonal = [att4[:, :, 8 * j : 8 * j + 8, 8 * j : 8 * j + 8] for j in range(2)]
            for j in range(2):
                nc.vector.tensor_tensor(out=weighted[:, :, j], in0=grad3, in1=diagonal[j], op=ALU.mult)
            for j in range(2):
                nc.vector.tensor_reduce(out=rowsum[:, j], in_=weighted[:, :, j], axis=AXIS_X, op=ALU.add)
            for j in range(2):
                half = att4[:, :, 8 * j : 8 * j + 8, :]
                sums = rowsum[:, j].unsqueeze(3).to_broadcast([P, 2, 8, 16])
                nc.vector.tensor_tensor(out=half, in0=half, in1=sums, op=ALU.mult)
            for j in range(2):
                nc.vector.tensor_tensor(out=diagonal[j], in0=diagonal[j], in1=weighted[:, :, j], op=ALU.subtract)

        def sort_dsc(pair):
            c = pair % CHUNKS
            sorted_dsc = work.tile([P, 16, 2, 8, 2], F32, name="sorted_dsc", align_bytes=64)
            if pair < CHUNKS:
                src = att_sb[c][:].rearrange("p (b i j h) -> p i b h j", b=2, i=16, j=2)
            else:
                src = att_sb[c][:].rearrange("p (b j h m) -> p m b h j", b=2, j=2, h=8)
            if pair == 0:
                for j in range(2):
                    nc.vector.tensor_copy(out=sorted_dsc[:, 8 * j : 8 * j + 8], in_=src[:, 8 * j : 8 * j + 8])
            else:
                nc.scalar.copy(out=sorted_dsc[:], in_=src)
            return sorted_dsc

        def turn_dsc(sorted_dsc):
            turned_dsc = work.tile([P, 512], F32, name="turned_dsc", align_bytes=64)
            nc.vector.transpose(out=turned_dsc[:], in_=sorted_dsc[:].rearrange("p x b h j -> p (x b h j)"))
            return turned_dsc

        def order_dsc(turned_dsc):
            ordered = work.tile([P, 32, 4, 4], F32, name="ordered")
            nc.vector.tensor_copy(
                out=ordered[:].rearrange("p G e (l j) -> p e G l j", j=2),
                in_=turned_dsc[:].rearrange("p (j l e G) -> p e G l j", j=2, l=2, e=4),
            )
            return ordered

        def build_blocks(blocks, ordered, tokens, groups, token_mask):
            for k in tokens:
                nc.vector.tensor_scalar(
                    out=blocks[:, groups, :, k, :],
                    in0=ordered[:, groups, :, :],
                    scalar1=token_mask[:, k : k + 1],
                    scalar2=None,
                    op0=ALU.mult,
                )

        def new_blocks():
            return work.tile([P, 32, 4, 8, 4], F32, name="blocks", align_bytes=64)

        def quantize(mx, cols, src, fmt):
            nc.vector.quantize_mx(out=mx[0][:, cols].bitcast(fmt), scales=mx[1][:, cols], in_=src)

        def mx_operand(name, width):
            codes = keep.tile([P, width], U32, name=name + "_codes", align_bytes=64)
            scales = keep.tile([P, width], U8, name=name + "_scales", align_bytes=64)
            return codes, scales

        w_mx = [mx_operand("w%d" % n, C) for n in range(4)]
        x_mx = [mx_operand("x%d" % g, C) for g in range(2)]
        token_mx = [mx_operand("token%d" % g, DIM) for g in range(2)]
        dq_mx = [mx_operand("dq%d" % c, 512) for c in range(CHUNKS)]
        dk_mx = [mx_operand("dk%d" % u, 256) for u in range(TILES)]
        dyq = [keep.tile([P, 2, 1024], F32, name="dyq%d" % g, align_bytes=64) for g in range(2)]
        dyk = {}
        token_side = keep.tile([P, 4, 256, 4], BF16, align_bytes=64)

        x_rows = x.rearrange("b n c -> (b n) c")
        inputs = [
            (w[K_PASS * l : K_PASS * (l + 1), :], "p (v u) c -> p c u v", w_mx[2 * n + l])
            for n, w in enumerate((Wq, Wk))
            for l in range(2)
        ]
        inputs.extend((x_rows[K_PASS * g : K_PASS * (g + 1), :], "p (u v) c -> p c u v", x_mx[g]) for g in range(2))
        raw = {}
        grouped = {}

        def load_input(n):
            raw[n] = work.tile([P, 4, C], BF16, name="raw")
            nc.sync.dma_start(out=raw[n][:], in_=inputs[n][0].rearrange("(p r) c -> p r c", r=4))

        def interleave(n, half, copy):
            grouped[n, half] = work.tile([P, N_TILE, 2, 2], BF16, name="grouped", align_bytes=64, bufs=3)
            src = raw[n][:, :, half * N_TILE : (half + 1) * N_TILE]
            copy(out=grouped[n, half][:], in_=src.rearrange(inputs[n][1], u=2))

        def quantize_input(n, half):
            src = grouped[n, half][:].rearrange("p c u v -> p (c u v)")
            quantize(inputs[n][2], slice(half * N_TILE, (half + 1) * N_TILE), src, E4M3)

        def sort_words(g, l):
            by_slot = work.tile([P, 2, 4, P], F32, name="by_slot")
            nc.vector.tensor_copy(out=by_slot[:], in_=dyq[g][:, l, :].rearrange("f (p r j) -> f j r p", r=4, j=2))
            return by_slot

        def turn_to_tokens(by_slot, l):
            for j in range(2):
                bank = mx_psum.tile([P, 4, P], F32, name="bank")
                for r in range(4):
                    nc.tensor.transpose(bank[:, r, :], by_slot[:, j, r, :], ident[:])
                nc.scalar.copy(
                    out=token_side[:, 2 * l + j, :, :],
                    in_=bank[:].rearrange("p r n -> p (r n)").bitcast(BF16).rearrange("p (r n) -> p n r", r=4),
                )

        def quantize_token_side(g, l):
            src = token_side[:, 2 * l : 2 * l + 2, :, :].rearrange("p j n r -> p (j n r)")
            quantize(token_mx[g], slice(512 * l, 512 * l + 512), src, E5M2)

        dx_rows = out_0.rearrange("b n c -> (b n) c")
        dw_rows = out_1.rearrange("(l s n j) c -> l j s n c", l=2, s=2, j=2)
        held = {}

        def mx_pass(operands, dst, half, n, after_products):
            cols = slice(half * N_TILE, (half + 1) * N_TILE)
            lhs, lhs_cols, rhs = operands[n]
            last = n == len(operands) - 1
            if n == 0:
                held["sums"] = mx_psum.tile([P, N_TILE], F32, name="bank")
            nc.tensor.matmul_mx(
                out=held["sums"][:],
                lhsT=lhs[0][:, lhs_cols].bitcast(E5M2),
                lhsT_scale=lhs[1][:, lhs_cols],
                rhs=rhs[0][:, cols].bitcast(E4M3),
                rhs_scale=rhs[1][:, cols],
                start=(n == 0),
                stop=last,
            )
            if last:
                if half == 0:
                    held["result"] = stage.tile([P, C], F32, name="result")
                copy = nc.vector.tensor_copy if half == 1 and after_products else nc.scalar.copy
                copy(out=held["result"][:, cols], in_=held["sums"][:])
                if after_products:
                    nc.sync.dma_start(out=dst[:, cols], in_=held["result"][:, cols])
                elif half == 1:
                    nc.sync.dma_start(out=dst, in_=held["result"][:])

        def passes_of(operands, dst):
            return [partial(mx_pass, operands, dst, half, n) for half in range(2) for n in range(len(operands))]

        def dx_passes(u):
            c, second = divmod(u, 2)
            operands = [(dq_mx[c], slice(256 * l + P * second, 256 * l + P * second + P), w_mx[l]) for l in range(2)]
            operands.extend((dk_mx[u], slice(P * l, P * l + P), w_mx[2 + l]) for l in range(2))
            return passes_of(operands, dx_rows[P * u : P * u + P, :])

        def dw_passes(u):
            operands = [(token_mx[g], slice(P * u, P * u + P), x_mx[g]) for g in range(2)]
            return passes_of(operands, dw_rows[u // 4, (u // 2) % 2, u % 2])

        mx_queue = []
        for u in range(TILES):
            if u >= 4:
                mx_queue.extend(dw_passes(2 * (u - 4)) + dw_passes(2 * (u - 4) + 1))
            mx_queue.extend(dx_passes(u))

        def product_bank(blocks, n, bank, rounded):
            sums = product_psum.tile([P, 8, D], F32, name="sums")
            for slot in range(8):
                group = 8 * bank + slot
                nc.tensor.matmul(
                    out=sums[:, slot, :],
                    lhsT=blocks[:, 16 * (n % 2) + group].rearrange("p e k u -> p (e k u)"),
                    rhs=rows_of[n][:, group, 0:128:2],
                    start=True,
                    stop=True,
                )
                if 2 * n + bank >= MX_FIRST_BANK:
                    mx_queue.pop(0)(False)
            dst = rounded[:, 512 * bank : 512 * bank + 512]
            src = sums[:].rearrange("p g d -> p (g d)")
            if n < TILES:
                nc.scalar.activation(out=dst, in_=src, func=ACT.Copy, scale=row_factor[:, 0:1])
            else:
                nc.scalar.copy(out=dst, in_=src)

        def turn_tile(rounded):
            turned = work.tile([P, 512], F32, name="turned", align_bytes=64)
            nc.vector.transpose(out=turned[:], in_=rounded[:].bitcast(F32))
            return turned

        def place_tile(n, turned):
            if n < TILES:
                dst = dyq[n // 4][:, :, 256 * (n % 4) : 256 * (n % 4) + 256]
            else:
                dyk[n - TILES] = work.tile([P, 2, 256], F32, name="dyk", align_bytes=64)
                dst = dyk[n - TILES][:]
            nc.vector.tensor_copy(
                out=dst.rearrange("p l (t j) -> p l t j", j=2),
                in_=turned[:].rearrange("p (t l j) -> p l t j", l=2, j=2),
            )

        def quantize_tile(n):
            if n >= TILES:
                src = dyk[n - TILES][:].rearrange("p l n -> p (l n)").bitcast(BF16)
                quantize(dk_mx[n - TILES], slice(0, 256), src, E5M2)
            elif n % 2 == 1:
                c = n // 2
                for l in range(2):
                    src = dyq[c // 2][:, l, 512 * (c % 2) : 512 * (c % 2) + 512].bitcast(BF16)
                    quantize(dq_mx[c], slice(256 * l, 256 * l + 256), src, E5M2)

        mask = keep.tile([P, 8], F32)
        nc.vector.tensor_reduce(out=mask[:], in_=ident[:].rearrange("p (k r) -> p k r", r=16), axis=AXIS_X, op=ALU.add)
        odd = keep.tile([P, 1], F32)
        nc.vector.tensor_reduce(out=odd[:], in_=ident[:, 1:P:2], axis=AXIS_X, op=ALU.add)
        even_factor = keep.tile([P, 1], F32)
        nc.vector.tensor_scalar(out=even_factor[:], in0=odd[:], scalar1=-1.0, scalar2=SCALE, op0=ALU.add, op1=ALU.mult)

        softmax_backward(0)
        sorted_dsc = sort_dsc(0)
        warm_up = mx_psum.tile([P, N_TILE], F32, name="bank")
        nc.tensor.matmul(
            out=warm_up[:],
            lhsT=ident[:],
            rhs=sorted_dsc[:].rearrange("p x b h j -> p (x b h j)"),
            start=True,
            stop=True,
        )
        ordered = order_dsc(turn_dsc(sorted_dsc))
        blocks = new_blocks()
        build_blocks(blocks, ordered, range(8), slice(0, 8), mask)
        build_blocks(blocks, ordered, range(8), slice(8, 16), mask)

        lam_products = keep.tile([P, 2, D], F32)
        for n in range(2):
            nc.vector.tensor_tensor(
                out=lam_products[:, n, :], in0=lam_vectors[2 * n][:], in1=lam_vectors[2 * n + 1][:], op=ALU.mult
            )
        lam_sums = keep.tile([P, 2], F32)
        nc.vector.tensor_reduce(out=lam_sums[:], in_=lam_products[:], axis=AXIS_X, op=ALU.add)
        lam_exps = keep.tile([P, 2], F32)
        nc.scalar.activation(out=lam_exps[:], in_=lam_sums[:], func=ACT.Exp)
        softmax_backward(1)
        sorted_dsc = sort_dsc(1)
        lam_difference = keep.tile([P, 1], F32)
        nc.vector.tensor_tensor(out=lam_difference[:], in0=lam_exps[:, 0:1], in1=lam_exps[:, 1:2], op=ALU.subtract)
        build_blocks(blocks, ordered, range(0, 4), slice(16, 32), mask)
        lam_scale = keep.tile([P, 1], F32)
        nc.vector.tensor_scalar(
            out=lam_scale[:], in0=lam_difference[:], scalar1=LAM_INIT, scalar2=SCALE, op0=ALU.add, op1=ALU.mult
        )
        build_blocks(blocks, ordered, range(4, 8), slice(16, 32), mask)
        row_factor = keep.tile([P, 1], F32)
        nc.vector.scalar_tensor_tensor(
            out=row_factor[:], in0=odd[:], scalar=lam_scale[:, 0:1], in1=even_factor[:], op0=ALU.mult, op1=ALU.add
        )
        turned_dsc = turn_dsc(sorted_dsc)
        scaled_mask = keep.tile([P, 8], F32)
        nc.vector.tensor_scalar(out=scaled_mask[:], in0=mask[:], scalar1=row_factor[:, 0:1], scalar2=None, op0=ALU.mult)
        ordered = order_dsc(turned_dsc)

        sort_at = {4 * g + 5 + l: (g, l) for g in range(2) for l in range(2)}
        turn_at = {n + 2: piece for n, piece in sort_at.items()}
        on_scalar = {}
        on_vector = {}
        for piece in range(8):
            n = W_FIRST_STEP + piece
            if n in turn_at:
                on_vector[n] = [divmod(piece, 2)]
            else:
                on_scalar[n] = divmod(piece, 2)
        for g in range(2):
            on_vector[X_FIRST_STEP + g] = [(4 + g, 0), (4 + g, 1)]
        load_at = {W_FIRST_STEP + 2 * n - 2: n for n in range(4)}
        load_at.update({X_FIRST_STEP + g - 2: 4 + g for g in range(2)})

        by_slot = {}
        all_groups = slice(0, 32)
        rounded = None
        for n in range(STEPS):
            pair = n // 2
            build = n % 2 == 0 and pair + 1 < TILES
            prepare = n % 2 == 1 and pair + 2 < TILES
            if n + ROWS_AHEAD < STEPS:
                load_rows(n + ROWS_AHEAD)
            if n in turn_at:
                turn_to_tokens(by_slot[turn_at[n]], turn_at[n][1])
            if build:
                next_blocks = new_blocks()
                next_mask = mask if pair + 1 < CHUNKS else scaled_mask
                build_blocks(next_blocks, ordered, range(0, 4), all_groups, next_mask)
            if prepare and pair + 2 < CHUNKS:
                softmax_backward(pair + 2)
            previous = rounded
            rounded = work.tile([P, 1024], BF16, name="rounded", align_bytes=64)
            product_bank(blocks, n, 0, rounded)
            if prepare:
                sorted_dsc = sort_dsc(pair + 2)
            product_bank(blocks, n, 1, rounded)
            if n in on_scalar:
                interleave(*on_scalar[n], nc.scalar.copy)
            if n > 0:
                turned = turn_tile(previous)
            if n in sort_at:
                by_slot[sort_at[n]] = sort_words(*sort_at[n])
            if build:
                build_blocks(next_blocks, ordered, range(4, 8), all_groups, next_mask)
            if n - 1 in on_scalar:
                quantize_input(*on_scalar[n - 1])
            if n > 0:
                place_tile(n - 1, turned)
            if prepare:
                turned_dsc = turn_dsc(sorted_dsc)
            for piece in on_vector.get(n, []):
                interleave(*piece, nc.vector.tensor_copy)
            if n - 1 in turn_at:
                quantize_token_side(*turn_at[n - 1])
            if n > 0:
                quantize_tile(n - 1)
            if prepare:
                ordered = order_dsc(turned_dsc)
            for piece in on_vector.get(n, []):
                quantize_input(*piece)
            if n in load_at:
                load_input(load_at[n])
            if n % 2 == 1:
                blocks = next_blocks

        place_tile(STEPS - 1, turn_tile(rounded))
        quantize_tile(STEPS - 1)
        for remaining in mx_queue:
            remaining(True)
